import numpy as np
import ml_dtypes


def mxq(x, axis, fmt="e4m3"):
    dtype, down = {"e4m3": (ml_dtypes.float8_e4m3fn, 7), "e5m2": (ml_dtypes.float8_e5m2, 14)}[fmt]
    v = np.moveaxis(np.asarray(x, np.float32).astype(ml_dtypes.bfloat16).astype(np.float64), axis, -1)
    blocks = v.reshape(v.shape[:-1] + (-1, 32))
    amax = np.abs(blocks).max(-1, keepdims=True)
    byte = np.maximum(np.where(amax > 0, np.frexp(amax)[1] - 1 + 127, 0) - down, 1)
    scale = np.exp2(byte - 127.0)
    codes = (blocks / scale).astype(np.float32).astype(dtype).astype(np.float64)
    return np.moveaxis((codes * scale).reshape(v.shape), -1, axis)


WIDE = False


def mx_kscale(k):
    if not WIDE:
        return np.ones(k)
    levels = np.array([10, -10, 5, -5, 0])
    a = np.random.permutation(np.resize(levels, k // 512 * 4)).reshape(k // 512, 4)
    idx = np.arange(k)
    return np.exp2(a[idx // 512, idx % 128 // 32])


BF16 = ml_dtypes.bfloat16


def bf(x):
    return np.asarray(x, np.float32).astype(BF16)


def f64(x):
    return np.asarray(x).astype(np.float64)


E2M1 = np.array([0.0, 0.5, 1.0, 1.5, 2.0, 3.0, 4.0, 6.0, -0.0, -0.5, -1.0, -1.5, -2.0, -3.0, -4.0, -6.0])


def pack_weight(w, fmt):
    k, n = w.shape
    w = f64(bf(w)).reshape(k // 32, 32, n)
    amax = np.abs(w).max(1)
    if fmt == "e4m3":
        byte = np.frexp(amax)[1] - 1 + 127 - 7
    else:
        mant, ex = np.frexp(amax / 6.0)
        byte = np.where(mant > 0.5, ex, ex - 1) + 127
    byte = np.clip(np.where(amax > 0, byte, 1), 1, 254)
    scaled = (w * np.exp2(127.0 - byte)[:, None, :]).reshape(k, n).astype(np.float32)
    by_word = np.ascontiguousarray(scaled.reshape(k // 512, 128, 4, n).transpose(0, 1, 3, 2))
    if fmt == "e4m3":
        words = by_word.astype(ml_dtypes.float8_e4m3fn).view(np.uint8)
    else:
        c = by_word.astype(ml_dtypes.float4_e2m1fn).view(np.uint8) & 0xF
        words = c[..., 0::2] | (c[..., 1::2] << 4)
    return np.ascontiguousarray(words), np.ascontiguousarray(byte.astype(np.uint8).reshape(k // 512, 16, n))


def unpack_weight(words, scales, fmt):
    g, p, n, _ = words.shape
    if fmt == "e4m3":
        vals = np.ascontiguousarray(words).view(ml_dtypes.float8_e4m3fn).astype(np.float64)
    else:
        nib = np.empty((g, p, n, 4), np.uint8)
        nib[..., 0::2] = words & 0xF
        nib[..., 1::2] = words >> 4
        vals = E2M1[nib]
    vals = vals * np.repeat(np.exp2(scales.astype(np.float64) - 127.0), 8, axis=1)[..., None]
    return vals.transpose(0, 1, 3, 2).reshape(g * 512, n)

def pack4(w):
    words, scales = pack_weight(w, "e2m1")
    return words.reshape(words.shape[0], 128, -1), scales


def unpack4(words, scales):
    return unpack_weight(words.reshape(words.shape[0], 128, -1, 2), scales, "e2m1")


S, D = 512, 2048
HALF = D // 2
BASE = 10000.0


def rope_interleaved(v):
    freqs = 1.0 / BASE ** (np.arange(HALF) / HALF)
    ang = np.arange(S)[:, None] * freqs[None, :]
    cos, sin = np.cos(ang), np.sin(ang)
    vp = v.reshape(S, HALF, 2)
    vr, vi = vp[..., 0], vp[..., 1]
    rot = np.stack([vr * cos - vi * sin, vr * sin + vi * cos], axis=-1)
    return rot.reshape(S, D)


def setup_inputs():
    s = mx_kscale(D)
    x = bf(np.random.standard_normal((S, D)) * s)
    w = np.random.standard_normal((D, D)) / np.sqrt(D) / s[None, :]
    words, scales = pack4(np.ascontiguousarray(w.T))
    return {"x": x, "w_words": words, "w_scales": scales}


def reference(x, w_words, w_scales):
    y = mxq(f64(x), 1, "e4m3") @ unpack4(w_words, w_scales)
    return rope_interleaved(y)

@@ -1,0 +1,264 @@
+import math
+from contextlib import ExitStack
+
+from concourse import mybir
+from concourse.masks import make_identity
+
+F32 = mybir.dt.float32
+BF16 = mybir.dt.bfloat16
+I32 = mybir.dt.int32
+U32 = mybir.dt.uint32
+U8 = mybir.dt.uint8
+FP8X4 = mybir.dt.float8_e4m3fn_x4
+FP4X4 = mybir.dt.float4_e2m1fn_x4
+ALU = mybir.AluOpType
+ACT = mybir.ActivationFunctionType
+
+S, D = 512, 2048
+HALF = D // 2
+BASE = 10000.0
+FLOPS = 2 * S * D * D
+
+P = 128
+PACK = 4
+K_PASS = P * PACK
+GROUPS = D // K_PASS
+ROW_TILES = S // P
+CHUNK = 512
+CHUNKS = D // CHUNK
+CHUNK_PAIRS = CHUNK // 2
+
+TWO_PI = 2.0 * math.pi
+ROUND_MAGIC = 1.5 * 2.0**23
+
+SIN_LIMIT = math.pi - 1e-3
+
+PRODUCTS_AHEAD = 8
+FOLD_AHEAD = 7
+TRIG_AHEAD = 6
+FLIP_AHEAD = 3
+QUANTISE_AHEAD = 2
+
+
+def bank_order():
+    banks = []
+    for d in range(ROW_TILES):
+        newest = CHUNKS - 1 - d
+        banks.extend([(d, c) for c in reversed(range(newest + 1, CHUNKS))])
+        banks.extend([(m, newest) for m in range(d + 1)])
+    return banks
+
+
+def angles_fit_sin(m, c):
+    largest = (m * P + P - 1) * BASE ** (-(c * CHUNK_PAIRS) / HALF)
+    return largest + math.pi / 2 < SIN_LIMIT
+
+
+def tile_ropeattention_pa_kernel(tc, x, w_words, w_scales, out):
+    nc = tc.nc
+    banks = bank_order()
+    first_use = [min([j for j, (m, c) in enumerate(banks) if m == tile]) for tile in range(ROW_TILES)]
+    late = banks[-ROW_TILES:]
+    early = [bank for bank in banks[:-ROW_TILES] if not angles_fit_sin(*bank)]
+    assert all([not angles_fit_sin(*bank) for bank in late])
+
+    with ExitStack() as ctx:
+        keep = ctx.enter_context(tc.tile_pool(name="keep", bufs=1))
+        stage = ctx.enter_context(tc.tile_pool(name="stage", bufs=2))
+        work = ctx.enter_context(tc.tile_pool(name="work", bufs=3))
+        done = ctx.enter_context(tc.tile_pool(name="done", bufs=4))
+        psum_x = ctx.enter_context(tc.psum_pool(name="psum_x", bufs=4))
+        psum_y = ctx.enter_context(tc.psum_pool(name="psum_y", bufs=4))
+        ctx.enter_context(tc.manual_schedule())
+
+        x_sb = keep.tile([P, ROW_TILES, D], BF16)
+        x_codes = keep.tile([P, ROW_TILES, GROUPS * P], U32, align_bytes=64)
+        x_scales = keep.tile([P, ROW_TILES, GROUPS * P], U8, align_bytes=64)
+        w_codes = keep.tile([P, GROUPS, 2 * D], U8, align_bytes=64)
+        w_planes = keep.tile([P, GROUPS, D], U8, align_bytes=64)
+        cos_t = keep.tile([P, ROW_TILES, HALF], F32)
+        sin_t = keep.tile([P, ROW_TILES, HALF], F32)
+        turns = keep.tile([P, ROW_TILES, HALF], F32)
+        whole = keep.tile([P, ROW_TILES, HALF], F32)
+        back = keep.tile([P, ROW_TILES, HALF], F32)
+        back_abs = keep.tile([P, ROW_TILES, HALF], F32)
+
+        row_i = keep.tile([P, ROW_TILES], I32)
+        nc.gpsimd.iota(row_i[:], pattern=[[P, ROW_TILES]], base=0, channel_multiplier=1)
+        nc.gpsimd.memset(w_planes[:].rearrange("p g n -> p (g n)").bitcast(F32), 0.0)
+        ident = keep.tile([P, P], F32)
+        make_identity(nc, ident[:])
+
+        freq = keep.tile([P, HALF], F32)
+        nc.vector.memset(freq[:, 0:1], 1.0)
+        width = 1
+        while width < HALF:
+            nc.vector.tensor_scalar(
+                out=freq[:, width : 2 * width],
+                in0=freq[:, 0:width],
+                scalar1=BASE ** (-width / HALF),
+                scalar2=None,
+                op0=ALU.mult,
+            )
+            width *= 2
+        row = keep.tile([P, ROW_TILES], F32)
+        nc.vector.tensor_copy(out=row[:], in_=row_i[:])
+        row_turns = keep.tile([P, ROW_TILES], F32)
+        nc.vector.tensor_scalar(out=row_turns[:], in0=row[:], scalar1=1.0 / TWO_PI, scalar2=None, op0=ALU.mult)
+        one = keep.tile([P, 1], F32)
+        nc.vector.memset(one[:], 1.0)
+        half_pi = keep.tile([P, 1], F32)
+        nc.vector.tensor_scalar(out=half_pi[:], in0=one[:], scalar1=math.pi / 2, scalar2=None, op0=ALU.mult)
+        magic = keep.tile([P, 1], F32)
+        nc.vector.memset(magic[:], ROUND_MAGIC)
+
+        def load_x(m):
+            nc.sync.dma_start(out=x_sb[:, m, :], in_=x[m * P : (m + 1) * P, :])
+
+        def load_w_scales():
+            for b in range(2):
+                for r in range(4):
+                    nc.sync.dma_start(
+                        out=w_planes[32 * b + r : P : 64, :, :].bitcast(I32),
+                        in_=w_scales[:, 4 * b + r : 16 : 8, :].rearrange("g j n -> j g n").bitcast(I32),
+                    )
+
+        def load_w_chunk(c):
+            cols = slice(2 * CHUNK * c, 2 * CHUNK * (c + 1))
+            nc.sync.dma_start(
+                out=w_codes[:, :, cols].bitcast(I32),
+                in_=w_words[:, :, cols].rearrange("g p b -> p g b").bitcast(I32),
+            )
+
+        load_x(0)
+        load_x(1)
+        load_w_scales()
+        for d in range(CHUNKS):
+            load_w_chunk(CHUNKS - 1 - d)
+            if d + 2 < ROW_TILES:
+                load_x(d + 2)
+
+        def pairs_of(c):
+            return slice(c * CHUNK_PAIRS, (c + 1) * CHUNK_PAIRS)
+
+        def products_on_vector(m, c):
+            cols = pairs_of(c)
+            per_row = row_turns[:, m : m + 1]
+            nc.vector.tensor_scalar(out=turns[:, m, cols], in0=freq[:, cols], scalar1=per_row, scalar2=None, op0=ALU.mult)
+            nc.vector.tensor_scalar(
+                out=whole[:, m, cols], in0=freq[:, cols], scalar1=per_row, scalar2=ROUND_MAGIC, op0=ALU.mult, op1=ALU.add
+            )
+
+        def products_on_scalar(m, c):
+            cols = pairs_of(c)
+            per_row = row_turns[:, m : m + 1]
+            nc.scalar.activation(out=turns[:, m, cols], in_=freq[:, cols], func=ACT.Copy, scale=per_row)
+            nc.scalar.activation(
+                out=whole[:, m, cols], in_=freq[:, cols], func=ACT.Identity, scale=per_row, bias=magic[:, 0:1]
+            )
+
+        def fold(m, c):
+            cols = pairs_of(c)
+            nc.vector.scalar_tensor_tensor(
+                out=back[:, m, cols],
+                in0=whole[:, m, cols],
+                scalar=ROUND_MAGIC,
+                in1=turns[:, m, cols],
+                op0=ALU.subtract,
+                op1=ALU.subtract,
+            )
+
+        def trig(m, c):
+            cols = pairs_of(c)
+            if angles_fit_sin(m, c):
+                per_row = row[:, m : m + 1]
+                nc.scalar.activation(out=sin_t[:, m, cols], in_=freq[:, cols], func=ACT.Sin, scale=per_row)
+                nc.scalar.activation(
+                    out=cos_t[:, m, cols], in_=freq[:, cols], func=ACT.Sin, scale=per_row, bias=half_pi[:, 0:1]
+                )
+            else:
+                nc.scalar.activation(out=back_abs[:, m, cols], in_=back[:, m, cols], func=ACT.Abs)
+                nc.scalar.activation(out=sin_t[:, m, cols], in_=back[:, m, cols], func=ACT.Sin, scale=-TWO_PI)
+                nc.scalar.activation(
+                    out=cos_t[:, m, cols], in_=back_abs[:, m, cols], func=ACT.Sin, scale=-TWO_PI, bias=half_pi[:, 0:1]
+                )
+
+        grouped_of = {}
+
+        def flip_x(m):
+            words = x_sb[:, m, :].bitcast(F32)
+            grouped = stage.tile([P, GROUPS * P * PACK], BF16, align_bytes=64)
+            grouped_of[m] = grouped
+            grouped_words = grouped[:].bitcast(F32).rearrange("p (g s u) -> p g s u", g=GROUPS, u=2)
+            for half in range(2):
+                flipped = psum_x.tile([P, 2, 2, P], F32)
+                for g2 in range(2):
+                    g = 2 * half + g2
+                    for u in range(2):
+                        nc.tensor.transpose(
+                            out=flipped[:, g2, u, :],
+                            in_=words[:, 256 * g + u : 256 * (g + 1) : 2],
+                            identity=ident[:],
+                        )
+                nc.scalar.copy(
+                    out=grouped_words[:, 2 * half : 2 * half + 2, :, :],
+                    in_=flipped[:].rearrange("p g u s -> p g s u"),
+                )
+
+        def quantise_x(m):
+            nc.vector.quantize_mx(
+                out=x_codes[:, m, :].bitcast(FP8X4), scales=x_scales[:, m, :], in_=grouped_of[m][:]
+            )
+
+        def project_and_rotate(m, c):
+            y = psum_y.tile([P, CHUNK_PAIRS, 2], F32)
+            for g in range(GROUPS):
+                rows = slice(g * P, (g + 1) * P)
+                nc.tensor.matmul_mx(
+                    out=y[:].rearrange("p i j -> p (i j)"),
+                    lhsT=x_codes[:, m, rows].bitcast(FP8X4),
+                    lhsT_scale=x_scales[:, m, rows],
+                    rhs=w_codes[:, g, 2 * CHUNK * c : 2 * CHUNK * (c + 1)].bitcast(FP4X4),
+                    rhs_scale=w_planes[:, g, CHUNK * c : CHUNK * (c + 1)],
+                    start=(g == 0),
+                    stop=(g == GROUPS - 1),
+                )
+            cos_c = cos_t[:, m, pairs_of(c)]
+            sin_c = sin_t[:, m, pairs_of(c)]
+            straight = work.tile([P, CHUNK_PAIRS, 2], F32)
+            nc.vector.tensor_tensor(
+                out=straight[:], in0=y[:], in1=cos_c.unsqueeze(2).to_broadcast([P, CHUNK_PAIRS, 2]), op=ALU.mult
+            )
+            crossed = work.tile([P, 2, CHUNK_PAIRS], F32)
+            nc.vector.scalar_tensor_tensor(
+                out=crossed[:, 0, :], in0=y[:, :, 1], scalar=-1.0, in1=sin_c, op0=ALU.mult, op1=ALU.mult
+            )
+            nc.vector.tensor_tensor(out=crossed[:, 1, :], in0=y[:, :, 0], in1=sin_c, op=ALU.mult)
+            rotated = done.tile([P, CHUNK_PAIRS, 2], F32)
+            nc.gpsimd.tensor_tensor(
+                out=rotated[:], in0=straight[:], in1=crossed[:].rearrange("p j i -> p i j"), op=ALU.add
+            )
+            nc.sync.dma_start(
+                out=out[m * P : (m + 1) * P, CHUNK * c : CHUNK * (c + 1)], in_=rotated[:].rearrange("p i j -> p (i j)")
+            )
+
+        for bank in early:
+            products_on_vector(*bank)
+        for bank in early:
+            fold(*bank)
+
+        for j in range(-TRIG_AHEAD, len(banks)):
+            if j + PRODUCTS_AHEAD < len(banks) and banks[j + PRODUCTS_AHEAD] in late:
+                products_on_scalar(*banks[j + PRODUCTS_AHEAD])
+            for m in range(ROW_TILES):
+                if first_use[m] == j + FLIP_AHEAD:
+                    flip_x(m)
+            if j + TRIG_AHEAD < len(banks):
+                trig(*banks[j + TRIG_AHEAD])
+            if j + FOLD_AHEAD < len(banks) and banks[j + FOLD_AHEAD] in late:
+                fold(*banks[j + FOLD_AHEAD])
+            for m in range(ROW_TILES):
+                if first_use[m] == j + QUANTISE_AHEAD:
+                    quantise_x(m)
+            if j >= 0:
+                project_and_rotate(*banks[j])

@@ -33,11 +33,14 @@ ROUND_MAGIC = 1.5 * 2.0**23
 
 SIN_LIMIT = math.pi - 1e-3
 
-PRODUCTS_AHEAD = 8
-FOLD_AHEAD = 7
+PRODUCTS_AHEAD = 15
+FOLD_AHEAD = 14
 TRIG_AHEAD = 6
 FLIP_AHEAD = 3
 QUANTISE_AHEAD = 2
+
+GPSIMD_PAIRS = 208
+assert GPSIMD_PAIRS % 4 == 0
 
 
 def bank_order():
@@ -51,22 +54,19 @@ def bank_order():
 
 def angles_fit_sin(m, c):
     largest = (m * P + P - 1) * BASE ** (-(c * CHUNK_PAIRS) / HALF)
-    return largest + math.pi / 2 < SIN_LIMIT
+    return largest < SIN_LIMIT
 
 
 def tile_ropeattention_pa_kernel(tc, x, w_words, w_scales, out):
     nc = tc.nc
     banks = bank_order()
     first_use = [min([j for j, (m, c) in enumerate(banks) if m == tile]) for tile in range(ROW_TILES)]
-    late = banks[-ROW_TILES:]
-    early = [bank for bank in banks[:-ROW_TILES] if not angles_fit_sin(*bank)]
-    assert all([not angles_fit_sin(*bank) for bank in late])
 
     with ExitStack() as ctx:
         keep = ctx.enter_context(tc.tile_pool(name="keep", bufs=1))
         stage = ctx.enter_context(tc.tile_pool(name="stage", bufs=2))
-        work = ctx.enter_context(tc.tile_pool(name="work", bufs=3))
-        done = ctx.enter_context(tc.tile_pool(name="done", bufs=4))
+        work = ctx.enter_context(tc.tile_pool(name="work", bufs=4))
+        done = ctx.enter_context(tc.tile_pool(name="done", bufs=6))
         psum_x = ctx.enter_context(tc.psum_pool(name="psum_x", bufs=4))
         psum_y = ctx.enter_context(tc.psum_pool(name="psum_y", bufs=4))
         ctx.enter_context(tc.manual_schedule())
@@ -74,7 +74,7 @@ def tile_ropeattention_pa_kernel(tc, x, w_words, w_scales, out):
         x_sb = keep.tile([P, ROW_TILES, D], BF16)
         x_codes = keep.tile([P, ROW_TILES, GROUPS * P], U32, align_bytes=64)
         x_scales = keep.tile([P, ROW_TILES, GROUPS * P], U8, align_bytes=64)
-        w_codes = keep.tile([P, GROUPS, 2 * D], U8, align_bytes=64)
+        w_codes = keep.tile([P, CHUNKS, GROUPS, 2 * CHUNK], U8, align_bytes=64)
         w_planes = keep.tile([P, GROUPS, D], U8, align_bytes=64)
         cos_t = keep.tile([P, ROW_TILES, HALF], F32)
         sin_t = keep.tile([P, ROW_TILES, HALF], F32)
@@ -103,14 +103,14 @@ def tile_ropeattention_pa_kernel(tc, x, w_words, w_scales, out):
             width *= 2
         row = keep.tile([P, ROW_TILES], F32)
         nc.vector.tensor_copy(out=row[:], in_=row_i[:])
+        row_neg = keep.tile([P, ROW_TILES], F32)
+        nc.vector.tensor_scalar(out=row_neg[:], in0=row[:], scalar1=-1.0, scalar2=None, op0=ALU.mult)
         row_turns = keep.tile([P, ROW_TILES], F32)
         nc.vector.tensor_scalar(out=row_turns[:], in0=row[:], scalar1=1.0 / TWO_PI, scalar2=None, op0=ALU.mult)
         one = keep.tile([P, 1], F32)
         nc.vector.memset(one[:], 1.0)
         half_pi = keep.tile([P, 1], F32)
         nc.vector.tensor_scalar(out=half_pi[:], in0=one[:], scalar1=math.pi / 2, scalar2=None, op0=ALU.mult)
-        magic = keep.tile([P, 1], F32)
-        nc.vector.memset(magic[:], ROUND_MAGIC)
 
         def load_x(m):
             nc.sync.dma_start(out=x_sb[:, m, :], in_=x[m * P : (m + 1) * P, :])
@@ -126,7 +126,7 @@ def tile_ropeattention_pa_kernel(tc, x, w_words, w_scales, out):
         def load_w_chunk(c):
             cols = slice(2 * CHUNK * c, 2 * CHUNK * (c + 1))
             nc.sync.dma_start(
-                out=w_codes[:, :, cols].bitcast(I32),
+                out=w_codes[:, c, :, :].bitcast(I32),
                 in_=w_words[:, :, cols].rearrange("g p b -> p g b").bitcast(I32),
             )
 
@@ -141,20 +141,12 @@ def tile_ropeattention_pa_kernel(tc, x, w_words, w_scales, out):
         def pairs_of(c):
             return slice(c * CHUNK_PAIRS, (c + 1) * CHUNK_PAIRS)
 
-        def products_on_vector(m, c):
+        def products(m, c):
             cols = pairs_of(c)
             per_row = row_turns[:, m : m + 1]
             nc.vector.tensor_scalar(out=turns[:, m, cols], in0=freq[:, cols], scalar1=per_row, scalar2=None, op0=ALU.mult)
             nc.vector.tensor_scalar(
                 out=whole[:, m, cols], in0=freq[:, cols], scalar1=per_row, scalar2=ROUND_MAGIC, op0=ALU.mult, op1=ALU.add
-            )
-
-        def products_on_scalar(m, c):
-            cols = pairs_of(c)
-            per_row = row_turns[:, m : m + 1]
-            nc.scalar.activation(out=turns[:, m, cols], in_=freq[:, cols], func=ACT.Copy, scale=per_row)
-            nc.scalar.activation(
-                out=whole[:, m, cols], in_=freq[:, cols], func=ACT.Identity, scale=per_row, bias=magic[:, 0:1]
             )
 
         def fold(m, c):
@@ -171,10 +163,13 @@ def tile_ropeattention_pa_kernel(tc, x, w_words, w_scales, out):
         def trig(m, c):
             cols = pairs_of(c)
             if angles_fit_sin(m, c):
-                per_row = row[:, m : m + 1]
-                nc.scalar.activation(out=sin_t[:, m, cols], in_=freq[:, cols], func=ACT.Sin, scale=per_row)
+                nc.scalar.activation(out=sin_t[:, m, cols], in_=freq[:, cols], func=ACT.Sin, scale=row[:, m : m + 1])
                 nc.scalar.activation(
-                    out=cos_t[:, m, cols], in_=freq[:, cols], func=ACT.Sin, scale=per_row, bias=half_pi[:, 0:1]
+                    out=cos_t[:, m, cols],
+                    in_=freq[:, cols],
+                    func=ACT.Sin,
+                    scale=row_neg[:, m : m + 1],
+                    bias=half_pi[:, 0:1],
                 )
             else:
                 nc.scalar.activation(out=back_abs[:, m, cols], in_=back[:, m, cols], func=ACT.Abs)
@@ -218,7 +213,7 @@ def tile_ropeattention_pa_kernel(tc, x, w_words, w_scales, out):
                     out=y[:].rearrange("p i j -> p (i j)"),
                     lhsT=x_codes[:, m, rows].bitcast(FP8X4),
                     lhsT_scale=x_scales[:, m, rows],
-                    rhs=w_codes[:, g, 2 * CHUNK * c : 2 * CHUNK * (c + 1)].bitcast(FP4X4),
+                    rhs=w_codes[:, c, g, :].bitcast(FP4X4),
                     rhs_scale=w_planes[:, g, CHUNK * c : CHUNK * (c + 1)],
                     start=(g == 0),
                     stop=(g == GROUPS - 1),
@@ -236,29 +231,47 @@ def tile_ropeattention_pa_kernel(tc, x, w_words, w_scales, out):
             nc.vector.tensor_tensor(out=crossed[:, 1, :], in0=y[:, :, 0], in1=sin_c, op=ALU.mult)
             rotated = done.tile([P, CHUNK_PAIRS, 2], F32)
             nc.gpsimd.tensor_tensor(
-                out=rotated[:], in0=straight[:], in1=crossed[:].rearrange("p j i -> p i j"), op=ALU.add
+                out=rotated[:, :GPSIMD_PAIRS, :],
+                in0=straight[:, :GPSIMD_PAIRS, :],
+                in1=crossed[:, :, :GPSIMD_PAIRS].rearrange("p j i -> p i j"),
+                op=ALU.add,
+            )
+            return straight, crossed, rotated
+
+        def finish_and_store(m, c, straight, crossed, rotated):
+            nc.vector.tensor_tensor(
+                out=rotated[:, GPSIMD_PAIRS:, :],
+                in0=straight[:, GPSIMD_PAIRS:, :],
+                in1=crossed[:, :, GPSIMD_PAIRS:].rearrange("p j i -> p i j"),
+                op=ALU.add,
             )
             nc.sync.dma_start(
                 out=out[m * P : (m + 1) * P, CHUNK * c : CHUNK * (c + 1)], in_=rotated[:].rearrange("p i j -> p (i j)")
             )
 
-        for bank in early:
-            products_on_vector(*bank)
-        for bank in early:
-            fold(*bank)
+        def bank_ahead(j, ahead):
+            return banks[j + ahead] if 0 <= j + ahead < len(banks) else None
 
-        for j in range(-TRIG_AHEAD, len(banks)):
-            if j + PRODUCTS_AHEAD < len(banks) and banks[j + PRODUCTS_AHEAD] in late:
-                products_on_scalar(*banks[j + PRODUCTS_AHEAD])
+        tiles_of = {}
+        for j in range(-PRODUCTS_AHEAD, len(banks) + 1):
+            bank = bank_ahead(j, PRODUCTS_AHEAD)
+            if bank is not None and not angles_fit_sin(*bank):
+                products(*bank)
             for m in range(ROW_TILES):
                 if first_use[m] == j + FLIP_AHEAD:
                     flip_x(m)
-            if j + TRIG_AHEAD < len(banks):
-                trig(*banks[j + TRIG_AHEAD])
-            if j + FOLD_AHEAD < len(banks) and banks[j + FOLD_AHEAD] in late:
-                fold(*banks[j + FOLD_AHEAD])
+            bank = bank_ahead(j, TRIG_AHEAD)
+            if bank is not None:
+                trig(*bank)
+            bank = bank_ahead(j, FOLD_AHEAD)
+            if bank is not None and not angles_fit_sin(*bank):
+                fold(*bank)
             for m in range(ROW_TILES):
                 if first_use[m] == j + QUANTISE_AHEAD:
                     quantise_x(m)
-            if j >= 0:
-                project_and_rotate(*banks[j])
+            bank = bank_ahead(j, 0)
+            if bank is not None:
+                tiles_of[bank] = project_and_rotate(*bank)
+            bank = bank_ahead(j, -1)
+            if bank is not None:
+                finish_and_store(*bank, *tiles_of[bank])

@@ -39,9 +39,6 @@ TRIG_AHEAD = 6
 FLIP_AHEAD = 3
 QUANTISE_AHEAD = 2
 
-GPSIMD_PAIRS = 208
-assert GPSIMD_PAIRS % 4 == 0
-
 
 def bank_order():
     banks = []
@@ -231,19 +228,7 @@ def tile_ropeattention_pa_kernel(tc, x, w_words, w_scales, out):
             nc.vector.tensor_tensor(out=crossed[:, 1, :], in0=y[:, :, 0], in1=sin_c, op=ALU.mult)
             rotated = done.tile([P, CHUNK_PAIRS, 2], F32)
             nc.gpsimd.tensor_tensor(
-                out=rotated[:, :GPSIMD_PAIRS, :],
-                in0=straight[:, :GPSIMD_PAIRS, :],
-                in1=crossed[:, :, :GPSIMD_PAIRS].rearrange("p j i -> p i j"),
-                op=ALU.add,
-            )
-            return straight, crossed, rotated
-
-        def finish_and_store(m, c, straight, crossed, rotated):
-            nc.vector.tensor_tensor(
-                out=rotated[:, GPSIMD_PAIRS:, :],
-                in0=straight[:, GPSIMD_PAIRS:, :],
-                in1=crossed[:, :, GPSIMD_PAIRS:].rearrange("p j i -> p i j"),
-                op=ALU.add,
+                out=rotated[:], in0=straight[:], in1=crossed[:].rearrange("p j i -> p i j"), op=ALU.add
             )
             nc.sync.dma_start(
                 out=out[m * P : (m + 1) * P, CHUNK * c : CHUNK * (c + 1)], in_=rotated[:].rearrange("p i j -> p (i j)")
@@ -252,8 +237,7 @@ def tile_ropeattention_pa_kernel(tc, x, w_words, w_scales, out):
         def bank_ahead(j, ahead):
             return banks[j + ahead] if 0 <= j + ahead < len(banks) else None
 
-        tiles_of = {}
-        for j in range(-PRODUCTS_AHEAD, len(banks) + 1):
+        for j in range(-PRODUCTS_AHEAD, len(banks)):
             bank = bank_ahead(j, PRODUCTS_AHEAD)
             if bank is not None and not angles_fit_sin(*bank):
                 products(*bank)
@@ -271,7 +255,4 @@ def tile_ropeattention_pa_kernel(tc, x, w_words, w_scales, out):
                     quantise_x(m)
             bank = bank_ahead(j, 0)
             if bank is not None:
-                tiles_of[bank] = project_and_rotate(*bank)
-            bank = bank_ahead(j, -1)
-            if bank is not None:
-                finish_and_store(*bank, *tiles_of[bank])
+                project_and_rotate(*bank)

@@ -28,16 +28,21 @@ CHUNK = 512
 CHUNKS = D // CHUNK
 CHUNK_PAIRS = CHUNK // 2
 
+DOUBLINGS = 10
+assert 2**DOUBLINGS == HALF
 TWO_PI = 2.0 * math.pi
 ROUND_MAGIC = 1.5 * 2.0**23
 
 SIN_LIMIT = math.pi - 1e-3
 
-PRODUCTS_AHEAD = 15
-FOLD_AHEAD = 14
+PRODUCTS_AHEAD = 10
+FOLD_AHEAD = 9
 TRIG_AHEAD = 6
 FLIP_AHEAD = 3
 QUANTISE_AHEAD = 2
+
+GPSIMD_PAIRS = 192
+assert GPSIMD_PAIRS % 4 == 0
 
 
 def bank_order():
@@ -82,14 +87,15 @@ def tile_ropeattention_pa_kernel(tc, x, w_words, w_scales, out):
 
         row_i = keep.tile([P, ROW_TILES], I32)
         nc.gpsimd.iota(row_i[:], pattern=[[P, ROW_TILES]], base=0, channel_multiplier=1)
-        nc.gpsimd.memset(w_planes[:].rearrange("p g n -> p (g n)").bitcast(F32), 0.0)
         ident = keep.tile([P, P], F32)
         make_identity(nc, ident[:])
 
         freq = keep.tile([P, HALF], F32)
         nc.vector.memset(freq[:, 0:1], 1.0)
-        width = 1
-        while width < HALF:
+        plane_words = w_planes[:].rearrange("p g n -> p (g n)").bitcast(I32)
+        slice_words = GROUPS * D // 4 // 8
+        for step in range(DOUBLINGS):
+            width = 2**step
             nc.vector.tensor_scalar(
                 out=freq[:, width : 2 * width],
                 in0=freq[:, 0:width],
@@ -97,7 +103,8 @@ def tile_ropeattention_pa_kernel(tc, x, w_words, w_scales, out):
                 scalar2=None,
                 op0=ALU.mult,
             )
-            width *= 2
+            if step < 8:
+                nc.vector.memset(plane_words[:, step * slice_words : (step + 1) * slice_words], 0)
         row = keep.tile([P, ROW_TILES], F32)
         nc.vector.tensor_copy(out=row[:], in_=row_i[:])
         row_neg = keep.tile([P, ROW_TILES], F32)
@@ -110,7 +117,9 @@ def tile_ropeattention_pa_kernel(tc, x, w_words, w_scales, out):
         nc.vector.tensor_scalar(out=half_pi[:], in0=one[:], scalar1=math.pi / 2, scalar2=None, op0=ALU.mult)
 
         def load_x(m):
-            nc.sync.dma_start(out=x_sb[:, m, :], in_=x[m * P : (m + 1) * P, :])
+            for half in range(2):
+                cols = slice(half * D // 2, (half + 1) * D // 2)
+                nc.sync.dma_start(out=x_sb[:, m, cols], in_=x[m * P : (m + 1) * P, cols])
 
         def load_w_scales():
             for b in range(2):
@@ -198,9 +207,13 @@ def tile_ropeattention_pa_kernel(tc, x, w_words, w_scales, out):
                 )
 
         def quantise_x(m):
-            nc.vector.quantize_mx(
-                out=x_codes[:, m, :].bitcast(FP8X4), scales=x_scales[:, m, :], in_=grouped_of[m][:]
-            )
+            for half in range(2):
+                rows = slice(half * 2 * P, (half + 1) * 2 * P)
+                nc.vector.quantize_mx(
+                    out=x_codes[:, m, rows].bitcast(FP8X4),
+                    scales=x_scales[:, m, rows],
+                    in_=grouped_of[m][:, half * 2 * P * PACK : (half + 1) * 2 * P * PACK],
+                )
 
         def project_and_rotate(m, c):
             y = psum_y.tile([P, CHUNK_PAIRS, 2], F32)
@@ -228,7 +241,19 @@ def tile_ropeattention_pa_kernel(tc, x, w_words, w_scales, out):
             nc.vector.tensor_tensor(out=crossed[:, 1, :], in0=y[:, :, 0], in1=sin_c, op=ALU.mult)
             rotated = done.tile([P, CHUNK_PAIRS, 2], F32)
             nc.gpsimd.tensor_tensor(
-                out=rotated[:], in0=straight[:], in1=crossed[:].rearrange("p j i -> p i j"), op=ALU.add
+                out=rotated[:, :GPSIMD_PAIRS, :],
+                in0=straight[:, :GPSIMD_PAIRS, :],
+                in1=crossed[:, :, :GPSIMD_PAIRS].rearrange("p j i -> p i j"),
+                op=ALU.add,
+            )
+            return straight, crossed, rotated
+
+        def finish_and_store(m, c, straight, crossed, rotated):
+            nc.vector.tensor_tensor(
+                out=rotated[:, GPSIMD_PAIRS:, :],
+                in0=straight[:, GPSIMD_PAIRS:, :],
+                in1=crossed[:, :, GPSIMD_PAIRS:].rearrange("p j i -> p i j"),
+                op=ALU.add,
             )
             nc.sync.dma_start(
                 out=out[m * P : (m + 1) * P, CHUNK * c : CHUNK * (c + 1)], in_=rotated[:].rearrange("p i j -> p (i j)")
@@ -237,7 +262,8 @@ def tile_ropeattention_pa_kernel(tc, x, w_words, w_scales, out):
         def bank_ahead(j, ahead):
             return banks[j + ahead] if 0 <= j + ahead < len(banks) else None
 
-        for j in range(-PRODUCTS_AHEAD, len(banks)):
+        tiles_of = {}
+        for j in range(-PRODUCTS_AHEAD, len(banks) + 1):
             bank = bank_ahead(j, PRODUCTS_AHEAD)
             if bank is not None and not angles_fit_sin(*bank):
                 products(*bank)
@@ -255,4 +281,7 @@ def tile_ropeattention_pa_kernel(tc, x, w_words, w_scales, out):
                     quantise_x(m)
             bank = bank_ahead(j, 0)
             if bank is not None:
-                project_and_rotate(*bank)
+                tiles_of[bank] = project_and_rotate(*bank)
+            bank = bank_ahead(j, -1)
+            if bank is not None:
+                finish_and_store(*bank, *tiles_of[bank])

@@ -31,7 +31,6 @@ CHUNK_PAIRS = CHUNK // 2
 DOUBLINGS = 10
 assert 2**DOUBLINGS == HALF
 TWO_PI = 2.0 * math.pi
-ROUND_MAGIC = 1.5 * 2.0**23
 
 SIN_LIMIT = math.pi - 1e-3
 
@@ -77,11 +76,10 @@ def tile_ropeattention_pa_kernel(tc, x, w_words, w_scales, out):
         x_codes = keep.tile([P, ROW_TILES, GROUPS * P], U32, align_bytes=64)
         x_scales = keep.tile([P, ROW_TILES, GROUPS * P], U8, align_bytes=64)
         w_codes = keep.tile([P, CHUNKS, GROUPS, 2 * CHUNK], U8, align_bytes=64)
-        w_planes = keep.tile([P, GROUPS, D], U8, align_bytes=64)
+        w_planes = [keep.tile([P, GROUPS, CHUNK], U8, align_bytes=64, name="w_planes%d" % c) for c in range(CHUNKS)]
         cos_t = keep.tile([P, ROW_TILES, HALF], F32)
         sin_t = keep.tile([P, ROW_TILES, HALF], F32)
-        turns = keep.tile([P, ROW_TILES, HALF], F32)
-        whole = keep.tile([P, ROW_TILES, HALF], F32)
+        whole = keep.tile([P, ROW_TILES, HALF], I32)
         back = keep.tile([P, ROW_TILES, HALF], F32)
         back_abs = keep.tile([P, ROW_TILES, HALF], F32)
 
@@ -92,8 +90,6 @@ def tile_ropeattention_pa_kernel(tc, x, w_words, w_scales, out):
 
         freq = keep.tile([P, HALF], F32)
         nc.vector.memset(freq[:, 0:1], 1.0)
-        plane_words = w_planes[:].rearrange("p g n -> p (g n)").bitcast(I32)
-        slice_words = GROUPS * D // 4 // 8
         for step in range(DOUBLINGS):
             width = 2**step
             nc.vector.tensor_scalar(
@@ -103,8 +99,8 @@ def tile_ropeattention_pa_kernel(tc, x, w_words, w_scales, out):
                 scalar2=None,
                 op0=ALU.mult,
             )
-            if step < 8:
-                nc.vector.memset(plane_words[:, step * slice_words : (step + 1) * slice_words], 0)
+            if step < CHUNKS:
+                nc.vector.memset(w_planes[CHUNKS - 1 - step][:].rearrange("p g n -> p (g n)").bitcast(I32), 0)
         row = keep.tile([P, ROW_TILES], F32)
         nc.vector.tensor_copy(out=row[:], in_=row_i[:])
         row_neg = keep.tile([P, ROW_TILES], F32)
@@ -121,15 +117,12 @@ def tile_ropeattention_pa_kernel(tc, x, w_words, w_scales, out):
                 cols = slice(half * D // 2, (half + 1) * D // 2)
                 nc.sync.dma_start(out=x_sb[:, m, cols], in_=x[m * P : (m + 1) * P, cols])
 
-        def load_w_scales():
-            for b in range(2):
-                for r in range(4):
-                    nc.sync.dma_start(
-                        out=w_planes[32 * b + r : P : 64, :, :].bitcast(I32),
-                        in_=w_scales[:, 4 * b + r : 16 : 8, :].rearrange("g j n -> j g n").bitcast(I32),
-                    )
-
         def load_w_chunk(c):
+            for r in range(4):
+                nc.sync.dma_start(
+                    out=w_planes[c][r:P:32, :, :].bitcast(I32),
+                    in_=w_scales[:, r:16:4, CHUNK * c : CHUNK * (c + 1)].rearrange("g j n -> j g n").bitcast(I32),
+                )
             cols = slice(2 * CHUNK * c, 2 * CHUNK * (c + 1))
             nc.sync.dma_start(
                 out=w_codes[:, c, :, :].bitcast(I32),
@@ -138,7 +131,6 @@ def tile_ropeattention_pa_kernel(tc, x, w_words, w_scales, out):
 
         load_x(0)
         load_x(1)
-        load_w_scales()
         for d in range(CHUNKS):
             load_w_chunk(CHUNKS - 1 - d)
             if d + 2 < ROW_TILES:
@@ -150,19 +142,16 @@ def tile_ropeattention_pa_kernel(tc, x, w_words, w_scales, out):
         def products(m, c):
             cols = pairs_of(c)
             per_row = row_turns[:, m : m + 1]
-            nc.vector.tensor_scalar(out=turns[:, m, cols], in0=freq[:, cols], scalar1=per_row, scalar2=None, op0=ALU.mult)
-            nc.vector.tensor_scalar(
-                out=whole[:, m, cols], in0=freq[:, cols], scalar1=per_row, scalar2=ROUND_MAGIC, op0=ALU.mult, op1=ALU.add
-            )
+            nc.vector.tensor_scalar(out=whole[:, m, cols], in0=freq[:, cols], scalar1=per_row, scalar2=None, op0=ALU.mult)
 
         def fold(m, c):
             cols = pairs_of(c)
             nc.vector.scalar_tensor_tensor(
                 out=back[:, m, cols],
-                in0=whole[:, m, cols],
-                scalar=ROUND_MAGIC,
-                in1=turns[:, m, cols],
-                op0=ALU.subtract,
+                in0=freq[:, cols],
+                scalar=row_turns[:, m : m + 1],
+                in1=whole[:, m, cols],
+                op0=ALU.mult,
                 op1=ALU.subtract,
             )
 
@@ -179,7 +168,7 @@ def tile_ropeattention_pa_kernel(tc, x, w_words, w_scales, out):
                 )
             else:
                 nc.scalar.activation(out=back_abs[:, m, cols], in_=back[:, m, cols], func=ACT.Abs)
-                nc.scalar.activation(out=sin_t[:, m, cols], in_=back[:, m, cols], func=ACT.Sin, scale=-TWO_PI)
+                nc.scalar.activation(out=sin_t[:, m, cols], in_=back[:, m, cols], func=ACT.Sin, scale=TWO_PI)
                 nc.scalar.activation(
                     out=cos_t[:, m, cols], in_=back_abs[:, m, cols], func=ACT.Sin, scale=-TWO_PI, bias=half_pi[:, 0:1]
                 )
@@ -224,7 +213,7 @@ def tile_ropeattention_pa_kernel(tc, x, w_words, w_scales, out):
                     lhsT=x_codes[:, m, rows].bitcast(FP8X4),
                     lhsT_scale=x_scales[:, m, rows],
                     rhs=w_codes[:, c, g, :].bitcast(FP4X4),
-                    rhs_scale=w_planes[:, g, CHUNK * c : CHUNK * (c + 1)],
+                    rhs_scale=w_planes[c][:, g, :],
                     start=(g == 0),
                     stop=(g == GROUPS - 1),
                 )

@@ -34,8 +34,6 @@ TWO_PI = 2.0 * math.pi
 
 SIN_LIMIT = math.pi - 1e-3
 
-PRODUCTS_AHEAD = 10
-FOLD_AHEAD = 9
 TRIG_AHEAD = 6
 FLIP_AHEAD = 3
 QUANTISE_AHEAD = 2
@@ -88,29 +86,36 @@ def tile_ropeattention_pa_kernel(tc, x, w_words, w_scales, out):
         ident = keep.tile([P, P], F32)
         make_identity(nc, ident[:])
 
+        row = keep.tile([P, ROW_TILES], F32)
+        row_neg = keep.tile([P, ROW_TILES], F32)
+        row_turns = keep.tile([P, ROW_TILES], F32)
+        one = keep.tile([P, 1], F32)
+        half_pi = keep.tile([P, 1], F32)
+
+        def zero_planes(c):
+            nc.vector.memset(w_planes[c][:].rearrange("p g n -> p (g n)").bitcast(I32), 0)
+
+        def scaled(out, in0, factor):
+            nc.vector.tensor_scalar(out=out, in0=in0, scalar1=factor, scalar2=None, op0=ALU.mult)
+
+        between = [
+            lambda: zero_planes(3),
+            lambda: nc.vector.tensor_copy(out=row[:], in_=row_i[:]),
+            lambda: zero_planes(2),
+            lambda: nc.vector.memset(one[:], 1.0),
+            lambda: scaled(row_turns[:], row[:], 1.0 / TWO_PI),
+            lambda: zero_planes(1),
+            lambda: scaled(row_neg[:], row[:], -1.0),
+            lambda: scaled(half_pi[:], one[:], math.pi / 2),
+            lambda: zero_planes(0),
+        ]
         freq = keep.tile([P, HALF], F32)
         nc.vector.memset(freq[:, 0:1], 1.0)
         for step in range(DOUBLINGS):
             width = 2**step
-            nc.vector.tensor_scalar(
-                out=freq[:, width : 2 * width],
-                in0=freq[:, 0:width],
-                scalar1=BASE ** (-width / HALF),
-                scalar2=None,
-                op0=ALU.mult,
-            )
-            if step < CHUNKS:
-                nc.vector.memset(w_planes[CHUNKS - 1 - step][:].rearrange("p g n -> p (g n)").bitcast(I32), 0)
-        row = keep.tile([P, ROW_TILES], F32)
-        nc.vector.tensor_copy(out=row[:], in_=row_i[:])
-        row_neg = keep.tile([P, ROW_TILES], F32)
-        nc.vector.tensor_scalar(out=row_neg[:], in0=row[:], scalar1=-1.0, scalar2=None, op0=ALU.mult)
-        row_turns = keep.tile([P, ROW_TILES], F32)
-        nc.vector.tensor_scalar(out=row_turns[:], in0=row[:], scalar1=1.0 / TWO_PI, scalar2=None, op0=ALU.mult)
-        one = keep.tile([P, 1], F32)
-        nc.vector.memset(one[:], 1.0)
-        half_pi = keep.tile([P, 1], F32)
-        nc.vector.tensor_scalar(out=half_pi[:], in0=one[:], scalar1=math.pi / 2, scalar2=None, op0=ALU.mult)
+            scaled(freq[:, width : 2 * width], freq[:, 0:width], BASE ** (-width / HALF))
+            if step < len(between):
+                between[step]()
 
         def load_x(m):
             for half in range(2):
@@ -139,13 +144,17 @@ def tile_ropeattention_pa_kernel(tc, x, w_words, w_scales, out):
         def pairs_of(c):
             return slice(c * CHUNK_PAIRS, (c + 1) * CHUNK_PAIRS)
 
-        def products(m, c):
-            cols = pairs_of(c)
-            per_row = row_turns[:, m : m + 1]
-            nc.vector.tensor_scalar(out=whole[:, m, cols], in0=freq[:, cols], scalar1=per_row, scalar2=None, op0=ALU.mult)
+        def folded_pairs(m):
+            unfit = [c for c in range(CHUNKS) if not angles_fit_sin(m, c)]
+            assert unfit == list(range(len(unfit)))
+            return slice(0, len(unfit) * CHUNK_PAIRS)
 
-        def fold(m, c):
-            cols = pairs_of(c)
+        def whole_turns(m):
+            cols = folded_pairs(m)
+            scaled(whole[:, m, cols], freq[:, cols], row_turns[:, m : m + 1])
+
+        def fold(m):
+            cols = folded_pairs(m)
             nc.vector.scalar_tensor_tensor(
                 out=back[:, m, cols],
                 in0=freq[:, cols],
@@ -204,6 +213,8 @@ def tile_ropeattention_pa_kernel(tc, x, w_words, w_scales, out):
                     in_=grouped_of[m][:, half * 2 * P * PACK : (half + 1) * 2 * P * PACK],
                 )
 
+        halves = [slice(0, CHUNK_PAIRS // 2), slice(CHUNK_PAIRS // 2, CHUNK_PAIRS)]
+
         def project_and_rotate(m, c):
             y = psum_y.tile([P, CHUNK_PAIRS, 2], F32)
             for g in range(GROUPS):
@@ -217,57 +228,74 @@ def tile_ropeattention_pa_kernel(tc, x, w_words, w_scales, out):
                     start=(g == 0),
                     stop=(g == GROUPS - 1),
                 )
-            cos_c = cos_t[:, m, pairs_of(c)]
-            sin_c = sin_t[:, m, pairs_of(c)]
+            last = (m, c) == banks[-1]
             straight = work.tile([P, CHUNK_PAIRS, 2], F32)
-            nc.vector.tensor_tensor(
-                out=straight[:], in0=y[:], in1=cos_c.unsqueeze(2).to_broadcast([P, CHUNK_PAIRS, 2]), op=ALU.mult
-            )
             crossed = work.tile([P, 2, CHUNK_PAIRS], F32)
-            nc.vector.scalar_tensor_tensor(
-                out=crossed[:, 0, :], in0=y[:, :, 1], scalar=-1.0, in1=sin_c, op0=ALU.mult, op1=ALU.mult
-            )
-            nc.vector.tensor_tensor(out=crossed[:, 1, :], in0=y[:, :, 0], in1=sin_c, op=ALU.mult)
             rotated = done.tile([P, CHUNK_PAIRS, 2], F32)
-            nc.gpsimd.tensor_tensor(
-                out=rotated[:, :GPSIMD_PAIRS, :],
-                in0=straight[:, :GPSIMD_PAIRS, :],
-                in1=crossed[:, :, :GPSIMD_PAIRS].rearrange("p j i -> p i j"),
-                op=ALU.add,
-            )
+            for part in halves if last else [slice(0, CHUNK_PAIRS)]:
+                first_pair = c * CHUNK_PAIRS
+                cos_c = cos_t[:, m, first_pair + part.start : first_pair + part.stop]
+                sin_c = sin_t[:, m, first_pair + part.start : first_pair + part.stop]
+                nc.vector.tensor_tensor(
+                    out=straight[:, part, :],
+                    in0=y[:, part, :],
+                    in1=cos_c.unsqueeze(2).to_broadcast([P, part.stop - part.start, 2]),
+                    op=ALU.mult,
+                )
+                nc.vector.scalar_tensor_tensor(
+                    out=crossed[:, 0, part], in0=y[:, part, 1], scalar=-1.0, in1=sin_c, op0=ALU.mult, op1=ALU.mult
+                )
+                nc.vector.tensor_tensor(out=crossed[:, 1, part], in0=y[:, part, 0], in1=sin_c, op=ALU.mult)
+            if not last:
+                add_up(nc.gpsimd, straight, crossed, rotated, slice(0, GPSIMD_PAIRS))
             return straight, crossed, rotated
 
-        def finish_and_store(m, c, straight, crossed, rotated):
-            nc.vector.tensor_tensor(
-                out=rotated[:, GPSIMD_PAIRS:, :],
-                in0=straight[:, GPSIMD_PAIRS:, :],
-                in1=crossed[:, :, GPSIMD_PAIRS:].rearrange("p j i -> p i j"),
+        def add_up(engine, straight, crossed, rotated, part):
+            engine.tensor_tensor(
+                out=rotated[:, part, :],
+                in0=straight[:, part, :],
+                in1=crossed[:, :, part].rearrange("p j i -> p i j"),
                 op=ALU.add,
             )
-            nc.sync.dma_start(
-                out=out[m * P : (m + 1) * P, CHUNK * c : CHUNK * (c + 1)], in_=rotated[:].rearrange("p i j -> p (i j)")
-            )
+
+        def finish_and_store(m, c, straight, crossed, rotated):
+            rows = slice(m * P, (m + 1) * P)
+            if (m, c) == banks[-1]:
+                for part in halves:
+                    add_up(nc.vector, straight, crossed, rotated, part)
+                    nc.sync.dma_start(
+                        out=out[rows, CHUNK * c + 2 * part.start : CHUNK * c + 2 * part.stop],
+                        in_=rotated[:, part, :].rearrange("p i j -> p (i j)"),
+                    )
+            else:
+                add_up(nc.vector, straight, crossed, rotated, slice(GPSIMD_PAIRS, CHUNK_PAIRS))
+                nc.sync.dma_start(out=out[rows, CHUNK * c : CHUNK * (c + 1)], in_=rotated[:].rearrange("p i j -> p (i j)"))
 
         def bank_ahead(j, ahead):
             return banks[j + ahead] if 0 <= j + ahead < len(banks) else None
 
+        def first_folded_bank(tile):
+            return min([j for j, (m, c) in enumerate(banks) if m == tile and not angles_fit_sin(m, c)])
+
+        fold_order = sorted(range(ROW_TILES), key=first_folded_bank)
+        for m in range(ROW_TILES):
+            whole_turns(m)
+        fold(fold_order[0])
+        fold(fold_order[1])
+
         tiles_of = {}
-        for j in range(-PRODUCTS_AHEAD, len(banks) + 1):
-            bank = bank_ahead(j, PRODUCTS_AHEAD)
-            if bank is not None and not angles_fit_sin(*bank):
-                products(*bank)
+        for j in range(-TRIG_AHEAD, len(banks) + 1):
             for m in range(ROW_TILES):
                 if first_use[m] == j + FLIP_AHEAD:
                     flip_x(m)
             bank = bank_ahead(j, TRIG_AHEAD)
             if bank is not None:
                 trig(*bank)
-            bank = bank_ahead(j, FOLD_AHEAD)
-            if bank is not None and not angles_fit_sin(*bank):
-                fold(*bank)
             for m in range(ROW_TILES):
                 if first_use[m] == j + QUANTISE_AHEAD:
                     quantise_x(m)
+                    if m + 2 < ROW_TILES:
+                        fold(fold_order[m + 2])
             bank = bank_ahead(j, 0)
             if bank is not None:
                 tiles_of[bank] = project_and_rotate(*bank)

@@ -51,9 +51,16 @@ def bank_order():
     return banks
 
 
+def largest_angle(m, c):
+    return (m * P + P - 1) * BASE ** (-(c * CHUNK_PAIRS) / HALF)
+
+
 def angles_fit_sin(m, c):
-    largest = (m * P + P - 1) * BASE ** (-(c * CHUNK_PAIRS) / HALF)
-    return largest < SIN_LIMIT
+    return largest_angle(m, c) < SIN_LIMIT
+
+
+def angles_need_folding(m, c):
+    return largest_angle(m, c) >= 2 * SIN_LIMIT
 
 
 def tile_ropeattention_pa_kernel(tc, x, w_words, w_scales, out):
@@ -91,24 +98,22 @@ def tile_ropeattention_pa_kernel(tc, x, w_words, w_scales, out):
         row_turns = keep.tile([P, ROW_TILES], F32)
         one = keep.tile([P, 1], F32)
         half_pi = keep.tile([P, 1], F32)
-
-        def zero_planes(c):
-            nc.vector.memset(w_planes[c][:].rearrange("p g n -> p (g n)").bitcast(I32), 0)
+        whole_pi = keep.tile([P, 1], F32)
+        half_pi_neg = keep.tile([P, 1], F32)
 
         def scaled(out, in0, factor):
             nc.vector.tensor_scalar(out=out, in0=in0, scalar1=factor, scalar2=None, op0=ALU.mult)
 
         between = [
-            lambda: zero_planes(3),
             lambda: nc.vector.tensor_copy(out=row[:], in_=row_i[:]),
-            lambda: zero_planes(2),
             lambda: nc.vector.memset(one[:], 1.0),
             lambda: scaled(row_turns[:], row[:], 1.0 / TWO_PI),
-            lambda: zero_planes(1),
-            lambda: scaled(row_neg[:], row[:], -1.0),
             lambda: scaled(half_pi[:], one[:], math.pi / 2),
-            lambda: zero_planes(0),
+            lambda: scaled(row_neg[:], row[:], -1.0),
+            lambda: scaled(whole_pi[:], one[:], math.pi),
+            lambda: scaled(half_pi_neg[:], one[:], -math.pi / 2),
         ]
+        assert len(between) < DOUBLINGS
         freq = keep.tile([P, HALF], F32)
         nc.vector.memset(freq[:, 0:1], 1.0)
         for step in range(DOUBLINGS):
@@ -145,7 +150,7 @@ def tile_ropeattention_pa_kernel(tc, x, w_words, w_scales, out):
             return slice(c * CHUNK_PAIRS, (c + 1) * CHUNK_PAIRS)
 
         def folded_pairs(m):
-            unfit = [c for c in range(CHUNKS) if not angles_fit_sin(m, c)]
+            unfit = [c for c in range(CHUNKS) if angles_need_folding(m, c)]
             assert unfit == list(range(len(unfit)))
             return slice(0, len(unfit) * CHUNK_PAIRS)
 
@@ -175,6 +180,15 @@ def tile_ropeattention_pa_kernel(tc, x, w_words, w_scales, out):
                     scale=row_neg[:, m : m + 1],
                     bias=half_pi[:, 0:1],
                 )
+            elif not angles_need_folding(m, c):
+                from_pi = back_abs[:, m, cols]
+                nc.scalar.activation(
+                    out=from_pi, in_=freq[:, cols], func=ACT.Abs, scale=row_neg[:, m : m + 1], bias=whole_pi[:, 0:1]
+                )
+                nc.scalar.activation(
+                    out=sin_t[:, m, cols], in_=freq[:, cols], func=ACT.Sin, scale=row_neg[:, m : m + 1], bias=whole_pi[:, 0:1]
+                )
+                nc.scalar.activation(out=cos_t[:, m, cols], in_=from_pi, func=ACT.Sin, bias=half_pi_neg[:, 0:1])
             else:
                 nc.scalar.activation(out=back_abs[:, m, cols], in_=back[:, m, cols], func=ACT.Abs)
                 nc.scalar.activation(out=sin_t[:, m, cols], in_=back[:, m, cols], func=ACT.Sin, scale=TWO_PI)
@@ -275,7 +289,7 @@ def tile_ropeattention_pa_kernel(tc, x, w_words, w_scales, out):
             return banks[j + ahead] if 0 <= j + ahead < len(banks) else None
 
         def first_folded_bank(tile):
-            return min([j for j, (m, c) in enumerate(banks) if m == tile and not angles_fit_sin(m, c)])
+            return min([j for j, (m, c) in enumerate(banks) if m == tile and angles_need_folding(m, c)])
 
         fold_order = sorted(range(ROW_TILES), key=first_folded_bank)
         for m in range(ROW_TILES):
@@ -283,14 +297,18 @@ def tile_ropeattention_pa_kernel(tc, x, w_words, w_scales, out):
         fold(fold_order[0])
         fold(fold_order[1])
 
+        trig(*banks[0])
+        tables_made = 1
+
         tiles_of = {}
-        for j in range(-TRIG_AHEAD, len(banks) + 1):
+        for j in range(-FLIP_AHEAD, len(banks) + 1):
             for m in range(ROW_TILES):
                 if first_use[m] == j + FLIP_AHEAD:
                     flip_x(m)
-            bank = bank_ahead(j, TRIG_AHEAD)
-            if bank is not None:
-                trig(*bank)
+            if j >= first_use[1] - FLIP_AHEAD + 1:
+                for bank in banks[tables_made : min(tables_made + 2, j + TRIG_AHEAD + 1)]:
+                    trig(*bank)
+                    tables_made += 1
             for m in range(ROW_TILES):
                 if first_use[m] == j + QUANTISE_AHEAD:
                     quantise_x(m)

@@ -37,6 +37,7 @@ SIN_LIMIT = math.pi - 1e-3
 TRIG_AHEAD = 6
 FLIP_AHEAD = 3
 QUANTISE_AHEAD = 2
+BUSY_AT_START = 5
 
 GPSIMD_PAIRS = 192
 assert GPSIMD_PAIRS % 4 == 0
@@ -73,7 +74,8 @@ def tile_ropeattention_pa_kernel(tc, x, w_words, w_scales, out):
         stage = ctx.enter_context(tc.tile_pool(name="stage", bufs=2))
         work = ctx.enter_context(tc.tile_pool(name="work", bufs=4))
         done = ctx.enter_context(tc.tile_pool(name="done", bufs=6))
-        psum_x = ctx.enter_context(tc.psum_pool(name="psum_x", bufs=4))
+        psum_x = ctx.enter_context(tc.psum_pool(name="psum_x", bufs=3))
+        psum_idle = ctx.enter_context(tc.psum_pool(name="psum_idle", bufs=1))
         psum_y = ctx.enter_context(tc.psum_pool(name="psum_y", bufs=4))
         ctx.enter_context(tc.manual_schedule())
 
@@ -87,6 +89,16 @@ def tile_ropeattention_pa_kernel(tc, x, w_words, w_scales, out):
         whole = keep.tile([P, ROW_TILES, HALF], I32)
         back = keep.tile([P, ROW_TILES, HALF], F32)
         back_abs = keep.tile([P, ROW_TILES, HALF], F32)
+
+        zeros = keep.tile([P, CHUNK], BF16)
+        nc.gpsimd.memset(zeros[:].bitcast(F32), 0.0)
+        unread = psum_idle.tile([P, CHUNK], F32)
+
+        def keep_busy(count):
+            for i in range(count):
+                nc.tensor.matmul(out=unread[:], lhsT=zeros[:, 0:P], rhs=zeros[:], start=True, stop=True)
+
+        keep_busy(BUSY_AT_START)
 
         row_i = keep.tile([P, ROW_TILES], I32)
         nc.gpsimd.iota(row_i[:], pattern=[[P, ROW_TILES]], base=0, channel_multiplier=1)
@@ -213,6 +225,8 @@ def tile_ropeattention_pa_kernel(tc, x, w_words, w_scales, out):
                             in_=words[:, 256 * g + u : 256 * (g + 1) : 2],
                             identity=ident[:],
                         )
+                if first_use[m] < FLIP_AHEAD:
+                    keep_busy(1)
                 nc.scalar.copy(
                     out=grouped_words[:, 2 * half : 2 * half + 2, :, :],
                     in_=flipped[:].rearrange("p g u s -> p g s u"),

@@ -28,8 +28,9 @@ CHUNK = 512
 CHUNKS = D // CHUNK
 CHUNK_PAIRS = CHUNK // 2
 
-DOUBLINGS = 10
-assert 2**DOUBLINGS == HALF
+DOUBLINGS = 4
+SEEDS = 2**DOUBLINGS
+assert SEEDS * SEEDS == CHUNK_PAIRS
 TWO_PI = 2.0 * math.pi
 
 SIN_LIMIT = math.pi - 1e-3
@@ -125,18 +126,31 @@ def tile_ropeattention_pa_kernel(tc, x, w_words, w_scales, out):
             lambda: scaled(whole_pi[:], one[:], math.pi),
             lambda: scaled(half_pi_neg[:], one[:], -math.pi / 2),
         ]
-        assert len(between) < DOUBLINGS
+        assert len(between) <= 2 * DOUBLINGS
         freq = keep.tile([P, HALF], F32)
-        nc.vector.memset(freq[:, 0:1], 1.0)
+        fine = keep.tile([P, SEEDS], F32)
+        coarse = keep.tile([P, SEEDS], F32)
+        nc.vector.memset(fine[:, 0:1], 1.0)
+        nc.vector.memset(coarse[:, 0:1], 1.0)
         for step in range(DOUBLINGS):
             width = 2**step
-            scaled(freq[:, width : 2 * width], freq[:, 0:width], BASE ** (-width / HALF))
-            if step < len(between):
-                between[step]()
+            scaled(fine[:, width : 2 * width], fine[:, 0:width], BASE ** (-width / HALF))
+            scaled(coarse[:, width : 2 * width], coarse[:, 0:width], BASE ** (-SEEDS * width / HALF))
+            for job in between[2 * step : 2 * step + 2]:
+                job()
+        nc.vector.tensor_tensor(
+            out=freq[:, 0:CHUNK_PAIRS].rearrange("p (a b) -> p a b", b=SEEDS),
+            in0=coarse[:].unsqueeze(2).to_broadcast([P, SEEDS, SEEDS]),
+            in1=fine[:].unsqueeze(1).to_broadcast([P, SEEDS, SEEDS]),
+            op=ALU.mult,
+        )
+        for c in reversed(range(1, CHUNKS)):
+            scaled(freq[:, c * CHUNK_PAIRS : (c + 1) * CHUNK_PAIRS], freq[:, 0:CHUNK_PAIRS], BASE ** (-c * CHUNK_PAIRS / HALF))
 
         def load_x(m):
-            for half in range(2):
-                cols = slice(half * D // 2, (half + 1) * D // 2)
+            pieces = 2 if m == 0 else 1
+            for piece in range(pieces):
+                cols = slice(piece * D // pieces, (piece + 1) * D // pieces)
                 nc.sync.dma_start(out=x_sb[:, m, cols], in_=x[m * P : (m + 1) * P, cols])
 
         def load_w_chunk(c):
@@ -326,8 +340,9 @@ def tile_ropeattention_pa_kernel(tc, x, w_words, w_scales, out):
             for m in range(ROW_TILES):
                 if first_use[m] == j + QUANTISE_AHEAD:
                     quantise_x(m)
-                    if m + 2 < ROW_TILES:
-                        fold(fold_order[m + 2])
+                    if m == 0:
+                        for tile in fold_order[2:]:
+                            fold(tile)
             bank = bank_ahead(j, 0)
             if bank is not None:
                 tiles_of[bank] = project_and_rotate(*bank)

@@ -35,7 +35,7 @@ TWO_PI = 2.0 * math.pi
 
 SIN_LIMIT = math.pi - 1e-3
 
-TRIG_AHEAD = 6
+TRIG_AHEAD = 3
 FLIP_AHEAD = 3
 QUANTISE_AHEAD = 2
 BUSY_AT_START = 5
@@ -86,7 +86,7 @@ def tile_ropeattention_pa_kernel(tc, x, w_words, w_scales, out):
         w_codes = keep.tile([P, CHUNKS, GROUPS, 2 * CHUNK], U8, align_bytes=64)
         w_planes = [keep.tile([P, GROUPS, CHUNK], U8, align_bytes=64, name="w_planes%d" % c) for c in range(CHUNKS)]
         cos_t = keep.tile([P, ROW_TILES, HALF], F32)
-        sin_t = keep.tile([P, ROW_TILES, HALF], F32)
+        sin_t = keep.tile([P, ROW_TILES, CHUNKS, 2, CHUNK_PAIRS], F32)
         whole = keep.tile([P, ROW_TILES, HALF], I32)
         back = keep.tile([P, ROW_TILES, HALF], F32)
         back_abs = keep.tile([P, ROW_TILES, HALF], F32)
@@ -113,6 +113,7 @@ def tile_ropeattention_pa_kernel(tc, x, w_words, w_scales, out):
         half_pi = keep.tile([P, 1], F32)
         whole_pi = keep.tile([P, 1], F32)
         half_pi_neg = keep.tile([P, 1], F32)
+        whole_pi_neg = keep.tile([P, 1], F32)
 
         def scaled(out, in0, factor):
             nc.vector.tensor_scalar(out=out, in0=in0, scalar1=factor, scalar2=None, op0=ALU.mult)
@@ -125,6 +126,7 @@ def tile_ropeattention_pa_kernel(tc, x, w_words, w_scales, out):
             lambda: scaled(row_neg[:], row[:], -1.0),
             lambda: scaled(whole_pi[:], one[:], math.pi),
             lambda: scaled(half_pi_neg[:], one[:], -math.pi / 2),
+            lambda: scaled(whole_pi_neg[:], one[:], -math.pi),
         ]
         assert len(between) <= 2 * DOUBLINGS
         freq = keep.tile([P, HALF], F32)
@@ -198,7 +200,8 @@ def tile_ropeattention_pa_kernel(tc, x, w_words, w_scales, out):
         def trig(m, c):
             cols = pairs_of(c)
             if angles_fit_sin(m, c):
-                nc.scalar.activation(out=sin_t[:, m, cols], in_=freq[:, cols], func=ACT.Sin, scale=row[:, m : m + 1])
+                nc.scalar.activation(out=sin_t[:, m, c, 1, :], in_=freq[:, cols], func=ACT.Sin, scale=row[:, m : m + 1])
+                nc.scalar.activation(out=sin_t[:, m, c, 0, :], in_=freq[:, cols], func=ACT.Sin, scale=row_neg[:, m : m + 1])
                 nc.scalar.activation(
                     out=cos_t[:, m, cols],
                     in_=freq[:, cols],
@@ -212,12 +215,16 @@ def tile_ropeattention_pa_kernel(tc, x, w_words, w_scales, out):
                     out=from_pi, in_=freq[:, cols], func=ACT.Abs, scale=row_neg[:, m : m + 1], bias=whole_pi[:, 0:1]
                 )
                 nc.scalar.activation(
-                    out=sin_t[:, m, cols], in_=freq[:, cols], func=ACT.Sin, scale=row_neg[:, m : m + 1], bias=whole_pi[:, 0:1]
+                    out=sin_t[:, m, c, 1, :], in_=freq[:, cols], func=ACT.Sin, scale=row_neg[:, m : m + 1], bias=whole_pi[:, 0:1]
+                )
+                nc.scalar.activation(
+                    out=sin_t[:, m, c, 0, :], in_=freq[:, cols], func=ACT.Sin, scale=row[:, m : m + 1], bias=whole_pi_neg[:, 0:1]
                 )
                 nc.scalar.activation(out=cos_t[:, m, cols], in_=from_pi, func=ACT.Sin, bias=half_pi_neg[:, 0:1])
             else:
                 nc.scalar.activation(out=back_abs[:, m, cols], in_=back[:, m, cols], func=ACT.Abs)
-                nc.scalar.activation(out=sin_t[:, m, cols], in_=back[:, m, cols], func=ACT.Sin, scale=TWO_PI)
+                nc.scalar.activation(out=sin_t[:, m, c, 1, :], in_=back[:, m, cols], func=ACT.Sin, scale=TWO_PI)
+                nc.scalar.activation(out=sin_t[:, m, c, 0, :], in_=back[:, m, cols], func=ACT.Sin, scale=-TWO_PI)
                 nc.scalar.activation(
                     out=cos_t[:, m, cols], in_=back_abs[:, m, cols], func=ACT.Sin, scale=-TWO_PI, bias=half_pi[:, 0:1]
                 )
@@ -277,17 +284,18 @@ def tile_ropeattention_pa_kernel(tc, x, w_words, w_scales, out):
             for part in halves if last else [slice(0, CHUNK_PAIRS)]:
                 first_pair = c * CHUNK_PAIRS
                 cos_c = cos_t[:, m, first_pair + part.start : first_pair + part.stop]
-                sin_c = sin_t[:, m, first_pair + part.start : first_pair + part.stop]
                 nc.vector.tensor_tensor(
                     out=straight[:, part, :],
                     in0=y[:, part, :],
                     in1=cos_c.unsqueeze(2).to_broadcast([P, part.stop - part.start, 2]),
                     op=ALU.mult,
                 )
-                nc.vector.scalar_tensor_tensor(
-                    out=crossed[:, 0, part], in0=y[:, part, 1], scalar=-1.0, in1=sin_c, op0=ALU.mult, op1=ALU.mult
+                nc.vector.tensor_tensor(
+                    out=crossed[:, :, part],
+                    in0=y[:, part, ::-1].rearrange("p i j -> p j i"),
+                    in1=sin_t[:, m, c, :, part],
+                    op=ALU.mult,
                 )
-                nc.vector.tensor_tensor(out=crossed[:, 1, part], in0=y[:, part, 0], in1=sin_c, op=ALU.mult)
             if not last:
                 add_up(nc.gpsimd, straight, crossed, rotated, slice(0, GPSIMD_PAIRS))
             return straight, crossed, rotated

@@ -38,18 +38,17 @@ SIN_LIMIT = math.pi - 1e-3
 TRIG_AHEAD = 3
 FLIP_AHEAD = 3
 QUANTISE_AHEAD = 2
-BUSY_AT_START = 5
+EARLY_TILES = 2
+BUSY_AT_START = 3
 
 GPSIMD_PAIRS = 192
 assert GPSIMD_PAIRS % 4 == 0
 
 
 def bank_order():
-    banks = []
-    for d in range(ROW_TILES):
-        newest = CHUNKS - 1 - d
-        banks.extend([(d, c) for c in reversed(range(newest + 1, CHUNKS))])
-        banks.extend([(m, newest) for m in range(d + 1)])
+    chunks = list(reversed(range(CHUNKS)))
+    banks = [(m, c) for c in chunks for m in range(EARLY_TILES)]
+    banks.extend([(m, c) for m in range(EARLY_TILES, ROW_TILES) for c in chunks])
     return banks
 
 
@@ -100,6 +99,9 @@ def tile_ropeattention_pa_kernel(tc, x, w_words, w_scales, out):
                 nc.tensor.matmul(out=unread[:], lhsT=zeros[:, 0:P], rhs=zeros[:], start=True, stop=True)
 
         keep_busy(BUSY_AT_START)
+
+        unread_sine = keep.tile([P, 1], F32)
+        nc.scalar.activation(out=unread_sine[:], in_=zeros[:, 0:1], func=ACT.Sin)
 
         row_i = keep.tile([P, ROW_TILES], I32)
         nc.gpsimd.iota(row_i[:], pattern=[[P, ROW_TILES]], base=0, channel_multiplier=1)
@@ -167,12 +169,12 @@ def tile_ropeattention_pa_kernel(tc, x, w_words, w_scales, out):
                 in_=w_words[:, :, cols].rearrange("g p b -> p g b").bitcast(I32),
             )
 
-        load_x(0)
-        load_x(1)
+        for m in range(EARLY_TILES):
+            load_x(m)
         for d in range(CHUNKS):
             load_w_chunk(CHUNKS - 1 - d)
-            if d + 2 < ROW_TILES:
-                load_x(d + 2)
+            if d >= ROW_TILES - EARLY_TILES:
+                load_x(d)
 
         def pairs_of(c):
             return slice(c * CHUNK_PAIRS, (c + 1) * CHUNK_PAIRS)
@@ -182,9 +184,16 @@ def tile_ropeattention_pa_kernel(tc, x, w_words, w_scales, out):
             assert unfit == list(range(len(unfit)))
             return slice(0, len(unfit) * CHUNK_PAIRS)
 
-        def whole_turns(m):
+        def whole_turns(m, engine):
             cols = folded_pairs(m)
-            scaled(whole[:, m, cols], freq[:, cols], row_turns[:, m : m + 1])
+            engine.tensor_scalar(
+                out=whole[:, m, cols],
+                in0=freq[:, cols],
+                scalar1=row_turns[:, m : m + 1],
+                scalar2=0.0,
+                op0=ALU.mult,
+                op1=ALU.add,
+            )
 
         def fold(m):
             cols = folded_pairs(m)
@@ -200,8 +209,6 @@ def tile_ropeattention_pa_kernel(tc, x, w_words, w_scales, out):
         def trig(m, c):
             cols = pairs_of(c)
             if angles_fit_sin(m, c):
-                nc.scalar.activation(out=sin_t[:, m, c, 1, :], in_=freq[:, cols], func=ACT.Sin, scale=row[:, m : m + 1])
-                nc.scalar.activation(out=sin_t[:, m, c, 0, :], in_=freq[:, cols], func=ACT.Sin, scale=row_neg[:, m : m + 1])
                 nc.scalar.activation(
                     out=cos_t[:, m, cols],
                     in_=freq[:, cols],
@@ -209,6 +216,8 @@ def tile_ropeattention_pa_kernel(tc, x, w_words, w_scales, out):
                     scale=row_neg[:, m : m + 1],
                     bias=half_pi[:, 0:1],
                 )
+                nc.scalar.activation(out=sin_t[:, m, c, 1, :], in_=freq[:, cols], func=ACT.Sin, scale=row[:, m : m + 1])
+                nc.scalar.activation(out=sin_t[:, m, c, 0, :], in_=freq[:, cols], func=ACT.Sin, scale=row_neg[:, m : m + 1])
             elif not angles_need_folding(m, c):
                 from_pi = back_abs[:, m, cols]
                 nc.scalar.activation(
@@ -328,13 +337,14 @@ def tile_ropeattention_pa_kernel(tc, x, w_words, w_scales, out):
             return min([j for j, (m, c) in enumerate(banks) if m == tile and angles_need_folding(m, c)])
 
         fold_order = sorted(range(ROW_TILES), key=first_folded_bank)
-        for m in range(ROW_TILES):
-            whole_turns(m)
-        fold(fold_order[0])
-        fold(fold_order[1])
+        for m in fold_order[EARLY_TILES:]:
+            whole_turns(m, nc.gpsimd)
+        for m in fold_order[:EARLY_TILES]:
+            whole_turns(m, nc.vector)
+        for m in fold_order[:EARLY_TILES]:
+            fold(m)
 
-        trig(*banks[0])
-        tables_made = 1
+        tables_made = 0
 
         tiles_of = {}
         for j in range(-FLIP_AHEAD, len(banks) + 1):
@@ -348,9 +358,8 @@ def tile_ropeattention_pa_kernel(tc, x, w_words, w_scales, out):
             for m in range(ROW_TILES):
                 if first_use[m] == j + QUANTISE_AHEAD:
                     quantise_x(m)
-                    if m == 0:
-                        for tile in fold_order[2:]:
-                            fold(tile)
+                    if m < EARLY_TILES:
+                        fold(fold_order[EARLY_TILES + m])
             bank = bank_ahead(j, 0)
             if bank is not None:
                 tiles_of[bank] = project_and_rotate(*bank)

@@ -39,7 +39,7 @@ TRIG_AHEAD = 3
 FLIP_AHEAD = 3
 QUANTISE_AHEAD = 2
 EARLY_TILES = 2
-BUSY_AT_START = 3
+BUSY_AT_START = 4
 
 GPSIMD_PAIRS = 192
 assert GPSIMD_PAIRS % 4 == 0

@@ -72,8 +72,7 @@ def tile_ropeattention_pa_kernel(tc, x, w_words, w_scales, out):
     with ExitStack() as ctx:
         keep = ctx.enter_context(tc.tile_pool(name="keep", bufs=1))
         stage = ctx.enter_context(tc.tile_pool(name="stage", bufs=2))
-        work = ctx.enter_context(tc.tile_pool(name="work", bufs=4))
-        done = ctx.enter_context(tc.tile_pool(name="done", bufs=6))
+        work = ctx.enter_context(tc.tile_pool(name="work", bufs=len(banks)))
         psum_x = ctx.enter_context(tc.psum_pool(name="psum_x", bufs=3))
         psum_idle = ctx.enter_context(tc.psum_pool(name="psum_idle", bufs=1))
         psum_y = ctx.enter_context(tc.psum_pool(name="psum_y", bufs=4))
@@ -86,9 +85,8 @@ def tile_ropeattention_pa_kernel(tc, x, w_words, w_scales, out):
         w_planes = [keep.tile([P, GROUPS, CHUNK], U8, align_bytes=64, name="w_planes%d" % c) for c in range(CHUNKS)]
         cos_t = keep.tile([P, ROW_TILES, HALF], F32)
         sin_t = keep.tile([P, ROW_TILES, CHUNKS, 2, CHUNK_PAIRS], F32)
-        whole = keep.tile([P, ROW_TILES, HALF], I32)
-        back = keep.tile([P, ROW_TILES, HALF], F32)
-        back_abs = keep.tile([P, ROW_TILES, HALF], F32)
+        whole = keep.tile([P, ROW_TILES, HALF // 2], I32)
+        back = keep.tile([P, ROW_TILES, HALF // 2], F32)
 
         zeros = keep.tile([P, CHUNK], BF16)
         nc.gpsimd.memset(zeros[:].bitcast(F32), 0.0)
@@ -206,37 +204,45 @@ def tile_ropeattention_pa_kernel(tc, x, w_words, w_scales, out):
                 op1=ALU.subtract,
             )
 
-        def trig(m, c):
+        def tables(m, c):
             cols = pairs_of(c)
+            cos_c = cos_t[:, m, cols]
+            sin_up = sin_t[:, m, c, 1, :]
+            sin_down = sin_t[:, m, c, 0, :]
+
+            def act(out, in_, func, **affine):
+                return lambda: nc.scalar.activation(out=out, in_=in_, func=func, **affine)
+
+            up = row[:, m : m + 1]
+            down = row_neg[:, m : m + 1]
             if angles_fit_sin(m, c):
-                nc.scalar.activation(
-                    out=cos_t[:, m, cols],
-                    in_=freq[:, cols],
-                    func=ACT.Sin,
-                    scale=row_neg[:, m : m + 1],
-                    bias=half_pi[:, 0:1],
+                return (
+                    lambda: None,
+                    act(cos_c, freq[:, cols], ACT.Sin, scale=down, bias=half_pi[:, 0:1]),
+                    act(sin_up, freq[:, cols], ACT.Sin, scale=up),
+                    act(sin_down, freq[:, cols], ACT.Sin, scale=down),
                 )
-                nc.scalar.activation(out=sin_t[:, m, c, 1, :], in_=freq[:, cols], func=ACT.Sin, scale=row[:, m : m + 1])
-                nc.scalar.activation(out=sin_t[:, m, c, 0, :], in_=freq[:, cols], func=ACT.Sin, scale=row_neg[:, m : m + 1])
-            elif not angles_need_folding(m, c):
-                from_pi = back_abs[:, m, cols]
-                nc.scalar.activation(
-                    out=from_pi, in_=freq[:, cols], func=ACT.Abs, scale=row_neg[:, m : m + 1], bias=whole_pi[:, 0:1]
+            if not angles_need_folding(m, c):
+                return (
+                    act(cos_c, freq[:, cols], ACT.Abs, scale=down, bias=whole_pi[:, 0:1]),
+                    act(cos_c, cos_c, ACT.Sin, bias=half_pi_neg[:, 0:1]),
+                    act(sin_up, freq[:, cols], ACT.Sin, scale=down, bias=whole_pi[:, 0:1]),
+                    act(sin_down, freq[:, cols], ACT.Sin, scale=up, bias=whole_pi_neg[:, 0:1]),
                 )
-                nc.scalar.activation(
-                    out=sin_t[:, m, c, 1, :], in_=freq[:, cols], func=ACT.Sin, scale=row_neg[:, m : m + 1], bias=whole_pi[:, 0:1]
-                )
-                nc.scalar.activation(
-                    out=sin_t[:, m, c, 0, :], in_=freq[:, cols], func=ACT.Sin, scale=row[:, m : m + 1], bias=whole_pi_neg[:, 0:1]
-                )
-                nc.scalar.activation(out=cos_t[:, m, cols], in_=from_pi, func=ACT.Sin, bias=half_pi_neg[:, 0:1])
-            else:
-                nc.scalar.activation(out=back_abs[:, m, cols], in_=back[:, m, cols], func=ACT.Abs)
-                nc.scalar.activation(out=sin_t[:, m, c, 1, :], in_=back[:, m, cols], func=ACT.Sin, scale=TWO_PI)
-                nc.scalar.activation(out=sin_t[:, m, c, 0, :], in_=back[:, m, cols], func=ACT.Sin, scale=-TWO_PI)
-                nc.scalar.activation(
-                    out=cos_t[:, m, cols], in_=back_abs[:, m, cols], func=ACT.Sin, scale=-TWO_PI, bias=half_pi[:, 0:1]
-                )
+            turn = back[:, m, cols]
+            return (
+                act(cos_c, turn, ACT.Abs),
+                act(cos_c, cos_c, ACT.Sin, scale=-TWO_PI, bias=half_pi[:, 0:1]),
+                act(sin_up, turn, ACT.Sin, scale=TWO_PI),
+                act(sin_down, turn, ACT.Sin, scale=-TWO_PI),
+            )
+
+        def trig(j):
+            none = (lambda: None,) * 4
+            cos_half, cos_end, unused, unused = tables(*banks[j]) if j < len(banks) else none
+            unused, unused, sin_up, sin_down = tables(*banks[j - 1]) if j > 0 else none
+            for job in (cos_half, sin_up, cos_end, sin_down):
+                job()
 
         grouped_of = {}
 
@@ -289,7 +295,7 @@ def tile_ropeattention_pa_kernel(tc, x, w_words, w_scales, out):
             last = (m, c) == banks[-1]
             straight = work.tile([P, CHUNK_PAIRS, 2], F32)
             crossed = work.tile([P, 2, CHUNK_PAIRS], F32)
-            rotated = done.tile([P, CHUNK_PAIRS, 2], F32)
+            rotated = work.tile([P, CHUNK_PAIRS, 2], F32)
             for part in halves if last else [slice(0, CHUNK_PAIRS)]:
                 first_pair = c * CHUNK_PAIRS
                 cos_c = cos_t[:, m, first_pair + part.start : first_pair + part.stop]
@@ -352,8 +358,8 @@ def tile_ropeattention_pa_kernel(tc, x, w_words, w_scales, out):
                 if first_use[m] == j + FLIP_AHEAD:
                     flip_x(m)
             if j >= first_use[1] - FLIP_AHEAD + 1:
-                for bank in banks[tables_made : min(tables_made + 2, j + TRIG_AHEAD + 1)]:
-                    trig(*bank)
+                for t in range(tables_made, min(tables_made + 2, j + TRIG_AHEAD + 1, len(banks) + 1)):
+                    trig(t)
                     tables_made += 1
             for m in range(ROW_TILES):
                 if first_use[m] == j + QUANTISE_AHEAD:

@@ -27,6 +27,7 @@ ROW_TILES = S // P
 CHUNK = 512
 CHUNKS = D // CHUNK
 CHUNK_PAIRS = CHUNK // 2
+PAIR = 2
 
 DOUBLINGS = 4
 SEEDS = 2**DOUBLINGS
@@ -82,7 +83,10 @@ def tile_ropeattention_pa_kernel(tc, x, w_words, w_scales, out):
         x_codes = keep.tile([P, ROW_TILES, GROUPS * P], U32, align_bytes=64)
         x_scales = keep.tile([P, ROW_TILES, GROUPS * P], U8, align_bytes=64)
         w_codes = keep.tile([P, CHUNKS, GROUPS, 2 * CHUNK], U8, align_bytes=64)
-        w_planes = [keep.tile([P, GROUPS, CHUNK], U8, align_bytes=64, name="w_planes%d" % c) for c in range(CHUNKS)]
+        plane_pairs = [
+            keep.tile([P, GROUPS, PAIR * CHUNK], U8, align_bytes=64, name="plane_pair%d" % pair) for pair in range(CHUNKS // PAIR)
+        ]
+        w_planes = [plane_pairs[c // PAIR][:, :, c % PAIR * CHUNK : (c % PAIR + 1) * CHUNK] for c in range(CHUNKS)]
         cos_t = keep.tile([P, ROW_TILES, HALF], F32)
         sin_t = keep.tile([P, ROW_TILES, CHUNKS, 2, CHUNK_PAIRS], F32)
         whole = keep.tile([P, ROW_TILES, HALF // 2], I32)
@@ -155,24 +159,34 @@ def tile_ropeattention_pa_kernel(tc, x, w_words, w_scales, out):
                 cols = slice(piece * D // pieces, (piece + 1) * D // pieces)
                 nc.sync.dma_start(out=x_sb[:, m, cols], in_=x[m * P : (m + 1) * P, cols])
 
-        def load_w_chunk(c):
+        def load_w_scales(pair):
+            cols = slice(pair * PAIR * CHUNK, (pair + 1) * PAIR * CHUNK)
             for r in range(4):
                 nc.sync.dma_start(
-                    out=w_planes[c][r:P:32, :, :].bitcast(I32),
-                    in_=w_scales[:, r:16:4, CHUNK * c : CHUNK * (c + 1)].rearrange("g j n -> j g n").bitcast(I32),
+                    out=plane_pairs[pair][r:P:32, :, :].bitcast(I32),
+                    in_=w_scales[:, r:16:4, cols].rearrange("g j n -> j g n").bitcast(I32),
                 )
-            cols = slice(2 * CHUNK * c, 2 * CHUNK * (c + 1))
-            nc.sync.dma_start(
-                out=w_codes[:, c, :, :].bitcast(I32),
-                in_=w_words[:, :, cols].rearrange("g p b -> p g b").bitcast(I32),
-            )
 
-        for m in range(EARLY_TILES):
-            load_x(m)
-        for d in range(CHUNKS):
-            load_w_chunk(CHUNKS - 1 - d)
-            if d >= ROW_TILES - EARLY_TILES:
-                load_x(d)
+        def load_w_codes(c):
+            pieces = 2 if c == CHUNKS - 1 else 1
+            cols = slice(2 * CHUNK * c, 2 * CHUNK * (c + 1))
+            for piece in range(pieces):
+                groups = slice(piece * GROUPS // pieces, (piece + 1) * GROUPS // pieces)
+                nc.sync.dma_start(
+                    out=w_codes[:, c, groups, :].bitcast(I32),
+                    in_=w_words[groups, :, cols].rearrange("g p b -> p g b").bitcast(I32),
+                )
+
+        load_x(0)
+        load_x(1)
+        load_w_scales(1)
+        load_w_codes(3)
+        load_w_codes(2)
+        load_w_codes(1)
+        load_w_scales(0)
+        load_x(2)
+        load_w_codes(0)
+        load_x(3)
 
         def pairs_of(c):
             return slice(c * CHUNK_PAIRS, (c + 1) * CHUNK_PAIRS)
@@ -261,7 +275,7 @@ def tile_ropeattention_pa_kernel(tc, x, w_words, w_scales, out):
                             in_=words[:, 256 * g + u : 256 * (g + 1) : 2],
                             identity=ident[:],
                         )
-                if first_use[m] < FLIP_AHEAD:
+                if m < EARLY_TILES and (m, half) != (EARLY_TILES - 1, 1):
                     keep_busy(1)
                 nc.scalar.copy(
                     out=grouped_words[:, 2 * half : 2 * half + 2, :, :],

@@ -36,7 +36,7 @@ TWO_PI = 2.0 * math.pi
 
 SIN_LIMIT = math.pi - 1e-3
 
-TRIG_AHEAD = 3
+TRIG_AHEAD = 2
 FLIP_AHEAD = 3
 QUANTISE_AHEAD = 2
 EARLY_TILES = 2
@@ -150,7 +150,7 @@ def tile_ropeattention_pa_kernel(tc, x, w_words, w_scales, out):
             in1=fine[:].unsqueeze(1).to_broadcast([P, SEEDS, SEEDS]),
             op=ALU.mult,
         )
-        for c in reversed(range(1, CHUNKS)):
+        for c in range(1, CHUNKS):
             scaled(freq[:, c * CHUNK_PAIRS : (c + 1) * CHUNK_PAIRS], freq[:, 0:CHUNK_PAIRS], BASE ** (-c * CHUNK_PAIRS / HALF))
 
         def load_x(m):
@@ -182,8 +182,8 @@ def tile_ropeattention_pa_kernel(tc, x, w_words, w_scales, out):
         load_w_scales(1)
         load_w_codes(3)
         load_w_codes(2)
-        load_w_codes(1)
         load_w_scales(0)
+        load_w_codes(1)
         load_x(2)
         load_w_codes(0)
         load_x(3)
@@ -195,6 +195,12 @@ def tile_ropeattention_pa_kernel(tc, x, w_words, w_scales, out):
             unfit = [c for c in range(CHUNKS) if angles_need_folding(m, c)]
             assert unfit == list(range(len(unfit)))
             return slice(0, len(unfit) * CHUNK_PAIRS)
+
+        def whole_on_scalar(m):
+            cols = folded_pairs(m)
+            nc.scalar.activation(
+                out=whole[:, m, cols].bitcast(U32), in_=freq[:, cols], func=ACT.Copy, scale=row_turns[:, m : m + 1]
+            )
 
         def whole_turns(m, engine):
             cols = folded_pairs(m)
@@ -357,11 +363,11 @@ def tile_ropeattention_pa_kernel(tc, x, w_words, w_scales, out):
             return min([j for j, (m, c) in enumerate(banks) if m == tile and angles_need_folding(m, c)])
 
         fold_order = sorted(range(ROW_TILES), key=first_folded_bank)
-        for m in fold_order[EARLY_TILES:]:
-            whole_turns(m, nc.gpsimd)
-        for m in fold_order[:EARLY_TILES]:
-            whole_turns(m, nc.vector)
-        for m in fold_order[:EARLY_TILES]:
+        whole_turns(fold_order[0], nc.vector)
+        whole_on_scalar(fold_order[1])
+        whole_on_scalar(fold_order[2])
+        whole_turns(fold_order[3], nc.gpsimd)
+        for m in fold_order[:3]:
             fold(m)
 
         tables_made = 0
@@ -369,20 +375,26 @@ def tile_ropeattention_pa_kernel(tc, x, w_words, w_scales, out):
         tiles_of = {}
         for j in range(-FLIP_AHEAD, len(banks) + 1):
             for m in range(ROW_TILES):
-                if first_use[m] == j + FLIP_AHEAD:
+                if m < EARLY_TILES and first_use[m] == j + FLIP_AHEAD:
                     flip_x(m)
             if j >= first_use[1] - FLIP_AHEAD + 1:
                 for t in range(tables_made, min(tables_made + 2, j + TRIG_AHEAD + 1, len(banks) + 1)):
                     trig(t)
                     tables_made += 1
             for m in range(ROW_TILES):
-                if first_use[m] == j + QUANTISE_AHEAD:
+                if m < EARLY_TILES and first_use[m] == j + QUANTISE_AHEAD:
                     quantise_x(m)
-                    if m < EARLY_TILES:
-                        fold(fold_order[EARLY_TILES + m])
+                    if m == 0:
+                        fold(fold_order[3])
             bank = bank_ahead(j, 0)
             if bank is not None:
                 tiles_of[bank] = project_and_rotate(*bank)
+            for m in range(EARLY_TILES, ROW_TILES):
+                if first_use[m] == j + 3:
+                    flip_x(m)
             bank = bank_ahead(j, -1)
             if bank is not None:
                 finish_and_store(*bank, *tiles_of[bank])
+            for m in range(EARLY_TILES, ROW_TILES):
+                if first_use[m] == j + 3:
+                    quantise_x(m)

import math
from contextlib import ExitStack

from concourse import mybir
from concourse.masks import make_identity

F32 = mybir.dt.float32
BF16 = mybir.dt.bfloat16
I32 = mybir.dt.int32
U32 = mybir.dt.uint32
U8 = mybir.dt.uint8
FP8X4 = mybir.dt.float8_e4m3fn_x4
FP4X4 = mybir.dt.float4_e2m1fn_x4
ALU = mybir.AluOpType
ACT = mybir.ActivationFunctionType

S, D = 512, 2048
HALF = D // 2
BASE = 10000.0
FLOPS = 2 * S * D * D

P = 128
PACK = 4
K_PASS = P * PACK
GROUPS = D // K_PASS
ROW_TILES = S // P
CHUNK = 512
CHUNKS = D // CHUNK
CHUNK_PAIRS = CHUNK // 2
PAIR = 2

DOUBLINGS = 4
SEEDS = 2**DOUBLINGS
assert SEEDS * SEEDS == CHUNK_PAIRS
TWO_PI = 2.0 * math.pi

SIN_LIMIT = math.pi - 1e-3

TRIG_AHEAD = 2
FLIP_AHEAD = 3
QUANTISE_AHEAD = 2
EARLY_TILES = 2
BUSY_AT_START = 4

GPSIMD_PAIRS = 192
assert GPSIMD_PAIRS % 4 == 0


def bank_order():
    chunks = list(reversed(range(CHUNKS)))
    banks = [(m, c) for c in chunks for m in range(EARLY_TILES)]
    banks.extend([(m, c) for m in range(EARLY_TILES, ROW_TILES) for c in chunks])
    return banks


def largest_angle(m, c):
    return (m * P + P - 1) * BASE ** (-(c * CHUNK_PAIRS) / HALF)


def angles_fit_sin(m, c):
    return largest_angle(m, c) < SIN_LIMIT


def angles_need_folding(m, c):
    return largest_angle(m, c) >= 2 * SIN_LIMIT


def tile_ropeattention_pa_kernel(tc, x, w_words, w_scales, out):
    nc = tc.nc
    banks = bank_order()
    first_use = [min([j for j, (m, c) in enumerate(banks) if m == tile]) for tile in range(ROW_TILES)]

    with ExitStack() as ctx:
        keep = ctx.enter_context(tc.tile_pool(name="keep", bufs=1))
        stage = ctx.enter_context(tc.tile_pool(name="stage", bufs=2))
        work = ctx.enter_context(tc.tile_pool(name="work", bufs=len(banks)))
        psum_x = ctx.enter_context(tc.psum_pool(name="psum_x", bufs=3))
        psum_idle = ctx.enter_context(tc.psum_pool(name="psum_idle", bufs=1))
        psum_y = ctx.enter_context(tc.psum_pool(name="psum_y", bufs=4))
        ctx.enter_context(tc.manual_schedule())

        x_sb = keep.tile([P, ROW_TILES, D], BF16)
        x_codes = keep.tile([P, ROW_TILES, GROUPS * P], U32, align_bytes=64)
        x_scales = keep.tile([P, ROW_TILES, GROUPS * P], U8, align_bytes=64)
        w_codes = keep.tile([P, CHUNKS, GROUPS, 2 * CHUNK], U8, align_bytes=64)
        plane_pairs = [
            keep.tile([P, GROUPS, PAIR * CHUNK], U8, align_bytes=64, name="plane_pair%d" % pair) for pair in range(CHUNKS // PAIR)
        ]
        w_planes = [plane_pairs[c // PAIR][:, :, c % PAIR * CHUNK : (c % PAIR + 1) * CHUNK] for c in range(CHUNKS)]
        cos_t = keep.tile([P, ROW_TILES, HALF], F32)
        sin_t = keep.tile([P, ROW_TILES, CHUNKS, 2, CHUNK_PAIRS], F32)
        whole = keep.tile([P, ROW_TILES, HALF // 2], I32)
        back = keep.tile([P, ROW_TILES, HALF // 2], F32)

        zeros = keep.tile([P, CHUNK], BF16)
        nc.gpsimd.memset(zeros[:].bitcast(F32), 0.0)
        unread = psum_idle.tile([P, CHUNK], F32)

        def keep_busy(count):
            for i in range(count):
                nc.tensor.matmul(out=unread[:], lhsT=zeros[:, 0:P], rhs=zeros[:], start=True, stop=True)

        keep_busy(BUSY_AT_START)

        unread_sine = keep.tile([P, 1], F32)
        nc.scalar.activation(out=unread_sine[:], in_=zeros[:, 0:1], func=ACT.Sin)

        row_i = keep.tile([P, ROW_TILES], I32)
        nc.gpsimd.iota(row_i[:], pattern=[[P, ROW_TILES]], base=0, channel_multiplier=1)
        ident = keep.tile([P, P], F32)
        make_identity(nc, ident[:])

        row = keep.tile([P, ROW_TILES], F32)
        row_neg = keep.tile([P, ROW_TILES], F32)
        row_turns = keep.tile([P, ROW_TILES], F32)
        one = keep.tile([P, 1], F32)
        half_pi = keep.tile([P, 1], F32)
        whole_pi = keep.tile([P, 1], F32)
        half_pi_neg = keep.tile([P, 1], F32)
        whole_pi_neg = keep.tile([P, 1], F32)

        def scaled(out, in0, factor):
            nc.vector.tensor_scalar(out=out, in0=in0, scalar1=factor, scalar2=None, op0=ALU.mult)

        between = [
            lambda: nc.vector.tensor_copy(out=row[:], in_=row_i[:]),
            lambda: nc.vector.memset(one[:], 1.0),
            lambda: scaled(row_turns[:], row[:], 1.0 / TWO_PI),
            lambda: scaled(half_pi[:], one[:], math.pi / 2),
            lambda: scaled(row_neg[:], row[:], -1.0),
            lambda: scaled(whole_pi[:], one[:], math.pi),
            lambda: scaled(half_pi_neg[:], one[:], -math.pi / 2),
            lambda: scaled(whole_pi_neg[:], one[:], -math.pi),
        ]
        assert len(between) <= 2 * DOUBLINGS
        freq = keep.tile([P, HALF], F32)
        fine = keep.tile([P, SEEDS], F32)
        coarse = keep.tile([P, SEEDS], F32)
        nc.vector.memset(fine[:, 0:1], 1.0)
        nc.vector.memset(coarse[:, 0:1], 1.0)
        for step in range(DOUBLINGS):
            width = 2**step
            scaled(fine[:, width : 2 * width], fine[:, 0:width], BASE ** (-width / HALF))
            scaled(coarse[:, width : 2 * width], coarse[:, 0:width], BASE ** (-SEEDS * width / HALF))
            for job in between[2 * step : 2 * step + 2]:
                job()
        nc.vector.tensor_tensor(
            out=freq[:, 0:CHUNK_PAIRS].rearrange("p (a b) -> p a b", b=SEEDS),
            in0=coarse[:].unsqueeze(2).to_broadcast([P, SEEDS, SEEDS]),
            in1=fine[:].unsqueeze(1).to_broadcast([P, SEEDS, SEEDS]),
            op=ALU.mult,
        )
        for c in range(1, CHUNKS):
            scaled(freq[:, c * CHUNK_PAIRS : (c + 1) * CHUNK_PAIRS], freq[:, 0:CHUNK_PAIRS], BASE ** (-c * CHUNK_PAIRS / HALF))

        def load_x(m):
            pieces = 2 if m == 0 else 1
            for piece in range(pieces):
                cols = slice(piece * D // pieces, (piece + 1) * D // pieces)
                nc.sync.dma_start(out=x_sb[:, m, cols], in_=x[m * P : (m + 1) * P, cols])

        def load_w_scales(pair):
            cols = slice(pair * PAIR * CHUNK, (pair + 1) * PAIR * CHUNK)
            for r in range(4):
                nc.sync.dma_start(
                    out=plane_pairs[pair][r:P:32, :, :].bitcast(I32),
                    in_=w_scales[:, r:16:4, cols].rearrange("g j n -> j g n").bitcast(I32),
                )

        def load_w_codes(c):
            pieces = 2 if c == CHUNKS - 1 else 1
            cols = slice(2 * CHUNK * c, 2 * CHUNK * (c + 1))
            for piece in range(pieces):
                groups = slice(piece * GROUPS // pieces, (piece + 1) * GROUPS // pieces)
                nc.sync.dma_start(
                    out=w_codes[:, c, groups, :].bitcast(I32),
                    in_=w_words[groups, :, cols].rearrange("g p b -> p g b").bitcast(I32),
                )

        load_x(0)
        load_x(1)
        load_w_scales(1)
        load_w_codes(3)
        load_w_codes(2)
        load_w_scales(0)
        load_w_codes(1)
        load_x(2)
        load_w_codes(0)
        load_x(3)

        def pairs_of(c):
            return slice(c * CHUNK_PAIRS, (c + 1) * CHUNK_PAIRS)

        def folded_pairs(m):
            unfit = [c for c in range(CHUNKS) if angles_need_folding(m, c)]
            assert unfit == list(range(len(unfit)))
            return slice(0, len(unfit) * CHUNK_PAIRS)

        def whole_on_scalar(m):
            cols = folded_pairs(m)
            nc.scalar.activation(
                out=whole[:, m, cols].bitcast(U32), in_=freq[:, cols], func=ACT.Copy, scale=row_turns[:, m : m + 1]
            )

        def whole_turns(m, engine):
            cols = folded_pairs(m)
            engine.tensor_scalar(
                out=whole[:, m, cols],
                in0=freq[:, cols],
                scalar1=row_turns[:, m : m + 1],
                scalar2=0.0,
                op0=ALU.mult,
                op1=ALU.add,
            )

        def fold(m):
            cols = folded_pairs(m)
            nc.vector.scalar_tensor_tensor(
                out=back[:, m, cols],
                in0=freq[:, cols],
                scalar=row_turns[:, m : m + 1],
                in1=whole[:, m, cols],
                op0=ALU.mult,
                op1=ALU.subtract,
            )

        def tables(m, c):
            cols = pairs_of(c)
            cos_c = cos_t[:, m, cols]
            sin_up = sin_t[:, m, c, 1, :]
            sin_down = sin_t[:, m, c, 0, :]

            def act(out, in_, func, **affine):
                return lambda: nc.scalar.activation(out=out, in_=in_, func=func, **affine)

            up = row[:, m : m + 1]
            down = row_neg[:, m : m + 1]
            if angles_fit_sin(m, c):
                return (
                    lambda: None,
                    act(cos_c, freq[:, cols], ACT.Sin, scale=down, bias=half_pi[:, 0:1]),
                    act(sin_up, freq[:, cols], ACT.Sin, scale=up),
                    act(sin_down, freq[:, cols], ACT.Sin, scale=down),
                )
            if not angles_need_folding(m, c):
                return (
                    act(cos_c, freq[:, cols], ACT.Abs, scale=down, bias=whole_pi[:, 0:1]),
                    act(cos_c, cos_c, ACT.Sin, bias=half_pi_neg[:, 0:1]),
                    act(sin_up, freq[:, cols], ACT.Sin, scale=down, bias=whole_pi[:, 0:1]),
                    act(sin_down, freq[:, cols], ACT.Sin, scale=up, bias=whole_pi_neg[:, 0:1]),
                )
            turn = back[:, m, cols]
            return (
                act(cos_c, turn, ACT.Abs),
                act(cos_c, cos_c, ACT.Sin, scale=-TWO_PI, bias=half_pi[:, 0:1]),
                act(sin_up, turn, ACT.Sin, scale=TWO_PI),
                act(sin_down, turn, ACT.Sin, scale=-TWO_PI),
            )

        def trig(j):
            none = (lambda: None,) * 4
            cos_half, cos_end, unused, unused = tables(*banks[j]) if j < len(banks) else none
            unused, unused, sin_up, sin_down = tables(*banks[j - 1]) if j > 0 else none
            for job in (cos_half, sin_up, cos_end, sin_down):
                job()

        grouped_of = {}

        def flip_x(m):
            words = x_sb[:, m, :].bitcast(F32)
            grouped = stage.tile([P, GROUPS * P * PACK], BF16, align_bytes=64)
            grouped_of[m] = grouped
            grouped_words = grouped[:].bitcast(F32).rearrange("p (g s u) -> p g s u", g=GROUPS, u=2)
            for half in range(2):
                flipped = psum_x.tile([P, 2, 2, P], F32)
                for g2 in range(2):
                    g = 2 * half + g2
                    for u in range(2):
                        nc.tensor.transpose(
                            out=flipped[:, g2, u, :],
                            in_=words[:, 256 * g + u : 256 * (g + 1) : 2],
                            identity=ident[:],
                        )
                if m < EARLY_TILES and (m, half) != (EARLY_TILES - 1, 1):
                    keep_busy(1)
                nc.scalar.copy(
                    out=grouped_words[:, 2 * half : 2 * half + 2, :, :],
                    in_=flipped[:].rearrange("p g u s -> p g s u"),
                )

        def quantise_x(m):
            for half in range(2):
                rows = slice(half * 2 * P, (half + 1) * 2 * P)
                nc.vector.quantize_mx(
                    out=x_codes[:, m, rows].bitcast(FP8X4),
                    scales=x_scales[:, m, rows],
                    in_=grouped_of[m][:, half * 2 * P * PACK : (half + 1) * 2 * P * PACK],
                )

        halves = [slice(0, CHUNK_PAIRS // 2), slice(CHUNK_PAIRS // 2, CHUNK_PAIRS)]

        def project_and_rotate(m, c):
            y = psum_y.tile([P, CHUNK_PAIRS, 2], F32)
            for g in range(GROUPS):
                rows = slice(g * P, (g + 1) * P)
                nc.tensor.matmul_mx(
                    out=y[:].rearrange("p i j -> p (i j)"),
                    lhsT=x_codes[:, m, rows].bitcast(FP8X4),
                    lhsT_scale=x_scales[:, m, rows],
                    rhs=w_codes[:, c, g, :].bitcast(FP4X4),
                    rhs_scale=w_planes[c][:, g, :],
                    start=(g == 0),
                    stop=(g == GROUPS - 1),
                )
            last = (m, c) == banks[-1]
            straight = work.tile([P, CHUNK_PAIRS, 2], F32)
            crossed = work.tile([P, 2, CHUNK_PAIRS], F32)
            rotated = work.tile([P, CHUNK_PAIRS, 2], F32)
            for part in halves if last else [slice(0, CHUNK_PAIRS)]:
                first_pair = c * CHUNK_PAIRS
                cos_c = cos_t[:, m, first_pair + part.start : first_pair + part.stop]
                nc.vector.tensor_tensor(
                    out=straight[:, part, :],
                    in0=y[:, part, :],
                    in1=cos_c.unsqueeze(2).to_broadcast([P, part.stop - part.start, 2]),
                    op=ALU.mult,
                )
                nc.vector.tensor_tensor(
                    out=crossed[:, :, part],
                    in0=y[:, part, ::-1].rearrange("p i j -> p j i"),
                    in1=sin_t[:, m, c, :, part],
                    op=ALU.mult,
                )
            if not last:
                add_up(nc.gpsimd, straight, crossed, rotated, slice(0, GPSIMD_PAIRS))
            return straight, crossed, rotated

        def add_up(engine, straight, crossed, rotated, part):
            engine.tensor_tensor(
                out=rotated[:, part, :],
                in0=straight[:, part, :],
                in1=crossed[:, :, part].rearrange("p j i -> p i j"),
                op=ALU.add,
            )

        def finish_and_store(m, c, straight, crossed, rotated):
            rows = slice(m * P, (m + 1) * P)
            if (m, c) == banks[-1]:
                for part in halves:
                    add_up(nc.vector, straight, crossed, rotated, part)
                    nc.sync.dma_start(
                        out=out[rows, CHUNK * c + 2 * part.start : CHUNK * c + 2 * part.stop],
                        in_=rotated[:, part, :].rearrange("p i j -> p (i j)"),
                    )
            else:
                add_up(nc.vector, straight, crossed, rotated, slice(GPSIMD_PAIRS, CHUNK_PAIRS))
                nc.sync.dma_start(out=out[rows, CHUNK * c : CHUNK * (c + 1)], in_=rotated[:].rearrange("p i j -> p (i j)"))

        def bank_ahead(j, ahead):
            return banks[j + ahead] if 0 <= j + ahead < len(banks) else None

        def first_folded_bank(tile):
            return min([j for j, (m, c) in enumerate(banks) if m == tile and angles_need_folding(m, c)])

        fold_order = sorted(range(ROW_TILES), key=first_folded_bank)
        whole_turns(fold_order[0], nc.vector)
        whole_on_scalar(fold_order[1])
        whole_on_scalar(fold_order[2])
        whole_turns(fold_order[3], nc.gpsimd)
        for m in fold_order[:3]:
            fold(m)

        tables_made = 0

        tiles_of = {}
        for j in range(-FLIP_AHEAD, len(banks) + 1):
            for m in range(ROW_TILES):
                if m < EARLY_TILES and first_use[m] == j + FLIP_AHEAD:
                    flip_x(m)
            if j >= first_use[1] - FLIP_AHEAD + 1:
                for t in range(tables_made, min(tables_made + 2, j + TRIG_AHEAD + 1, len(banks) + 1)):
                    trig(t)
                    tables_made += 1
            for m in range(ROW_TILES):
                if m < EARLY_TILES and first_use[m] == j + QUANTISE_AHEAD:
                    quantise_x(m)
                    if m == 0:
                        fold(fold_order[3])
            bank = bank_ahead(j, 0)
            if bank is not None:
                tiles_of[bank] = project_and_rotate(*bank)
            for m in range(EARLY_TILES, ROW_TILES):
                if first_use[m] == j + 3:
                    flip_x(m)
            bank = bank_ahead(j, -1)
            if bank is not None:
                finish_and_store(*bank, *tiles_of[bank])
            for m in range(EARLY_TILES, ROW_TILES):
                if first_use[m] == j + 3:
                    quantise_x(m)
